import numpy as np
import ml_dtypes


def mxq(x, axis, fmt="e4m3"):
    dtype, down = {"e4m3": (ml_dtypes.float8_e4m3fn, 7), "e5m2": (ml_dtypes.float8_e5m2, 14)}[fmt]
    v = np.moveaxis(np.asarray(x, np.float32).astype(ml_dtypes.bfloat16).astype(np.float64), axis, -1)
    blocks = v.reshape(v.shape[:-1] + (-1, 32))
    amax = np.abs(blocks).max(-1, keepdims=True)
    byte = np.maximum(np.where(amax > 0, np.frexp(amax)[1] - 1 + 127, 0) - down, 1)
    scale = np.exp2(byte - 127.0)
    codes = (blocks / scale).astype(np.float32).astype(dtype).astype(np.float64)
    return np.moveaxis((codes * scale).reshape(v.shape), -1, axis)


WIDE = False


def mx_kscale(k):
    if not WIDE:
        return np.ones(k)
    levels = np.array([10, -10, 5, -5, 0])
    a = np.random.permutation(np.resize(levels, k // 512 * 4)).reshape(k // 512, 4)
    idx = np.arange(k)
    return np.exp2(a[idx // 512, idx % 128 // 32])


BF16 = ml_dtypes.bfloat16


def bf(x):
    return np.asarray(x, np.float32).astype(BF16)


def f64(x):
    return np.asarray(x).astype(np.float64)


B, S, D, H, KA, LW = 8, 2048, 512, 128, 3, 2
G = KA + 1
M = S // G
QS = np.sqrt(2.0 * np.sqrt(D / H))


def sparse_causal_mask(n, ka):
    i = np.arange(n)[:, None]
    j = np.arange(n)[None, :]
    local = np.abs(j - i) <= LW
    atrous = ((j - i) % (ka + 1) == 0) & ~((j == 0) & (i > 0))
    return (local | atrous) & (j <= i)


def classes(t):
    return t.reshape(B, M, G, H).transpose(0, 2, 1, 3)


def setup_inputs():
    s = mx_kscale(D)
    return {"q": bf(np.random.standard_normal((B, S, H)) * QS),
            "k_proj": bf(np.random.standard_normal((B, S, H)) * QS),
            "x": bf(np.random.standard_normal((B, S, D)) * s),
            "Wv": bf(np.random.standard_normal((H, D)) / np.sqrt(D) / s)}


def reference(q, k_proj, x, Wv):
    q, k_proj = f64(q), f64(k_proj)
    v = mxq(f64(x), 2, "e4m3") @ mxq(f64(Wv), 1, "e4m3").T
    mask = sparse_causal_mask(S, KA)
    keep = np.stack([mask[r::G, r::G] for r in range(G)])
    sa = classes(q) @ classes(k_proj).transpose(0, 1, 3, 2) / np.sqrt(D)
    sa = np.where(keep, sa, -np.inf)
    sl = np.full((LW, B, S), -np.inf)
    for d in range(1, LW + 1):
        sl[d - 1, :, d:] = (q[:, d:] * k_proj[:, :-d]).sum(-1) / np.sqrt(D)
    top = np.maximum(sa.max(-1).transpose(0, 2, 1).reshape(B, S), sl.max(0))
    ea = np.exp(sa - top.reshape(B, M, G).transpose(0, 2, 1)[..., None])
    el = np.exp(sl - top)
    num = mxq(ea, 3, "e4m3") @ mxq(classes(v), 2, "e4m3")
    num = num.transpose(0, 2, 1, 3).reshape(B, S, H)
    loc = np.zeros((B, S, H))
    for d in range(1, LW + 1):
        loc[:, d:] += el[d - 1, :, d:, None] * v[:, :-d]
    den = ea.sum(-1).transpose(0, 2, 1).reshape(B, S) + el.sum(0)
    return (num + loc) / den[..., None]

@@ -1,0 +1,479 @@
+from contextlib import ExitStack
+import math
+
+import concourse.mybir as mybir
+from concourse.masks import make_identity
+
+F32 = mybir.dt.float32
+BF16 = mybir.dt.bfloat16
+U32 = mybir.dt.uint32
+U8 = mybir.dt.uint8
+FP8X4 = mybir.dt.float8_e4m3fn_x4
+ALU = mybir.AluOpType
+ACT = mybir.ActivationFunctionType
+AX = mybir.AxisListType
+
+B, S, D, H = 8, 2048, 512, 128
+P = 128
+PACK = 4
+R = 4
+LW = 2
+M = S // R
+J = M // P
+SCALE = 1.0 / math.sqrt(D)
+NEG = -1.0e30
+KPAD = 16
+
+CAUSAL = 0
+CAUSAL_NO_KEY0 = 1
+NO_KEY0 = 2
+N_MASKS = 3
+
+N_PARTS = B * J
+N_STEPS = B * R
+N_TILES = N_STEPS * J
+
+FLOPS = 2 * B * S * D * H + 2 * (2 * B * R * M * M * H)
+
+
+def tile_singlehead_pa_t_kernel(tc, q, k_proj, x, Wv, out):
+    nc = tc.nc
+    with ExitStack() as ctx:
+        ctx.enter_context(tc.manual_schedule())
+        const = ctx.enter_context(tc.tile_pool(name="const", bufs=1))
+        loads = ctx.enter_context(tc.tile_pool(name="loads", bufs=3))
+        whole = ctx.enter_context(tc.tile_pool(name="whole", bufs=2))
+        work = ctx.enter_context(tc.tile_pool(name="work", bufs=2))
+        small = ctx.enter_context(tc.tile_pool(name="small", bufs=4))
+        psum_s = ctx.enter_context(tc.psum_pool(name="psum_s", bufs=3))
+        psum_e = ctx.enter_context(tc.psum_pool(name="psum_e", bufs=2))
+        psum_o = ctx.enter_context(tc.psum_pool(name="psum_o", bufs=1))
+        psum_p = ctx.enter_context(tc.psum_pool(name="psum_p", bufs=2))
+
+        ident_f32 = const.tile([P, P], F32)
+        make_identity(nc, ident_f32[:])
+        ident_bf = const.tile([P, P], BF16)
+        make_identity(nc, ident_bf[:])
+
+        causal_f32 = const.tile([P, P], F32)
+        nc.gpsimd.memset(causal_f32[:], 0.0)
+        nc.gpsimd.affine_select(
+            out=causal_f32[:], in_=causal_f32[:], compare_op=ALU.is_ge, fill=NEG,
+            base=0, pattern=[[-1, P]], channel_multiplier=1,
+        )
+        mask_tiles = const.tile([P, N_MASKS, P], BF16)
+        nc.vector.tensor_copy(out=mask_tiles[:, CAUSAL, :], in_=causal_f32[:])
+        nc.vector.tensor_copy(out=mask_tiles[:, CAUSAL_NO_KEY0, :], in_=causal_f32[:])
+        nc.vector.memset(mask_tiles[:, CAUSAL_NO_KEY0, 0:1], NEG)
+        nc.vector.memset(mask_tiles[0:1, CAUSAL_NO_KEY0, 0:1], 0.0)
+        nc.vector.memset(mask_tiles[:, NO_KEY0, :], 0.0)
+        nc.vector.memset(mask_tiles[:, NO_KEY0, 0:1], NEG)
+
+        ones_f32 = const.tile([P, 2], F32)
+        nc.vector.memset(ones_f32[:], 1.0)
+        no_token = const.tile([P, LW, R, J], F32)
+        nc.vector.memset(no_token[:], 0.0)
+        for d in range(1, LW + 1):
+            nc.vector.memset(no_token[0:1, d - 1, 0:d, 0:1], -SCALE * NEG)
+
+        e_grouped_pair = [
+            const.tile([P, J, P, PACK], BF16, align_bytes=64, name="e_grouped_0"),
+            const.tile([P, J, P, PACK], BF16, align_bytes=64, name="e_grouped_1"),
+        ]
+        for e_grouped in e_grouped_pair:
+            nc.vector.memset(e_grouped[:], 0.0)
+
+        qk_t_pair = [
+            const.tile([P, 2, R, KPAD + M], BF16, name="qk_t_0"),
+            const.tile([P, 2, R, KPAD + M], BF16, name="qk_t_1"),
+        ]
+        for qk_t in qk_t_pair:
+            nc.vector.memset(qk_t[:, 1, :, 0:KPAD], 0.0)
+
+        def transpose_words(words_out, words_in):
+            for u in range(2):
+                nc.tensor.transpose(words_out[:, u, :], words_in[:, u, :], ident_f32[:])
+
+        wv_sb = const.tile([P, D], BF16)
+        nc.sync.dma_start(out=wv_sb[:], in_=Wv)
+        wv_t = psum_p.tile([P, 2, P], F32, tag="prep")
+        transpose_words(wv_t, wv_sb[:].bitcast(F32).rearrange("h (u w) -> h u w", u=2))
+        wv_grouped = const.tile([P, H * PACK], BF16, align_bytes=64)
+        nc.vector.tensor_copy(
+            out=wv_grouped[:].bitcast(F32).rearrange("w (h u) -> w h u", u=2),
+            in_=wv_t[:].rearrange("w u h -> w h u"),
+        )
+        wv_codes = const.tile([P, H], U32, align_bytes=64)
+        wv_scales = const.tile([P, H], U8, align_bytes=64)
+        nc.vector.quantize_mx(out=wv_codes[:].bitcast(FP8X4), scales=wv_scales[:], in_=wv_grouped[:])
+
+        seqs = {}
+        parts = {}
+        steps = {}
+        logit_tiles = {}
+        far_maxima = {}
+        e_tiles = {}
+
+        def load(part):
+            if not 0 <= part < N_PARTS:
+                return
+            b, g = divmod(part, J)
+            tokens = slice(g * R * P, (g + 1) * R * P)
+            qk_in = loads.tile([P, 2, R, H], BF16)
+            nc.sync.dma_start(out=qk_in[:, 0], in_=q[b, tokens, :].rearrange("(p r) h -> p r h", r=R))
+            nc.sync.dma_start(out=qk_in[:, 1], in_=k_proj[b, tokens, :].rearrange("(p r) h -> p r h", r=R))
+            x_in = loads.tile([P, R * D], BF16)
+            nc.sync.dma_start(out=x_in[:], in_=x[b, tokens, :].rearrange("(p r) d -> p (r d)", r=R))
+            parts[part] = dict(qk_in=qk_in, x_in=x_in)
+
+        def heads_to_partitions(part):
+            if not 0 <= part < N_PARTS:
+                return
+            b, g = divmod(part, J)
+            if g == 0:
+                seqs[b] = dict(
+                    qk_t=qk_t_pair[b % 2],
+                    v_near=whole.tile([P, J, LW + R, H], F32, name="v_near"),
+                    near=whole.tile([P, LW, R, J], F32, name="near"),
+                    near_min=whole.tile([P, R, J], F32, name="near_min"),
+                    o_sb=whole.tile([P, J, R, H], F32, name="o_sb"),
+                )
+            qk_in = parts[part]["qk_in"]
+            heads_t = psum_p.tile([P, 2, R, P], BF16, tag="prep")
+            for side in range(2):
+                for r in range(R):
+                    nc.tensor.transpose(heads_t[:, side, r, :], qk_in[:, side, r, :], ident_bf[:])
+            first = KPAD + g * P
+            nc.scalar.copy(out=seqs[b]["qk_t"][:, :, :, first : first + P], in_=heads_t[:])
+
+        def local_products(part):
+            if not 0 <= part < N_PARTS:
+                return
+            b, g = divmod(part, J)
+            qk_t = seqs[b]["qk_t"]
+            first = KPAD + g * P
+            products = work.tile([P, LW, R, P], F32)
+            for d in range(1, LW + 1):
+                nc.vector.tensor_tensor(
+                    out=products[:, d - 1, 0:d, :], in0=qk_t[:, 0, 0:d, first : first + P],
+                    in1=qk_t[:, 1, R - d : R, first - 1 : first - 1 + P], op=ALU.mult,
+                )
+                nc.vector.tensor_tensor(
+                    out=products[:, d - 1, d:R, :], in0=qk_t[:, 0, d:R, first : first + P],
+                    in1=qk_t[:, 1, 0 : R - d, first : first + P], op=ALU.mult,
+                )
+            parts[part]["products"] = products
+
+        def local_sums(part):
+            if not 0 <= part < N_PARTS:
+                return
+            near_ps = psum_p.tile([P, LW, R, 2], F32, tag="prep")
+            for d in range(LW):
+                for r in range(R):
+                    nc.tensor.matmul(
+                        out=near_ps[:, d, r, :], lhsT=parts[part]["products"][:, d, r, :],
+                        rhs=ones_f32[:], start=True, stop=True,
+                    )
+            parts[part]["near_ps"] = near_ps
+
+        def local_logits(part):
+            if not 0 <= part < N_PARTS:
+                return
+            b, g = divmod(part, J)
+            near = seqs[b]["near"]
+            nc.vector.scalar_tensor_tensor(
+                out=near[:, :, :, g], in0=parts[part]["near_ps"][:, :, :, 0], scalar=-SCALE,
+                in1=no_token[:, :, :, g], op0=ALU.mult, op1=ALU.add,
+            )
+
+        def local_minimum(part):
+            if not 0 <= part < N_PARTS:
+                return
+            b, g = divmod(part, J)
+            near = seqs[b]["near"]
+            nc.vector.tensor_tensor(
+                out=seqs[b]["near_min"][:, :, g], in0=near[:, 0, :, g], in1=near[:, 1, :, g], op=ALU.min
+            )
+
+        def x_to_partitions(part, pair):
+            if not 0 <= part < N_PARTS:
+                return
+            if pair == 0:
+                parts[part]["x_grouped"] = work.tile([P, R * P * PACK], BF16, align_bytes=64, name="x_grouped")
+            x_words = parts[part]["x_in"][:].bitcast(F32).rearrange("p (r u w) -> p r u w", r=R, u=2)
+            x_grouped_words = parts[part]["x_grouped"][:].bitcast(F32).rearrange("w (r p u) -> w r p u", r=R, p=P)
+            x_t = psum_p.tile([P, 2, 2, P], F32, tag="prep")
+            for c in range(2):
+                transpose_words(x_t[:, c], x_words[:, 2 * pair + c])
+            nc.scalar.copy(
+                out=x_grouped_words[:, 2 * pair : 2 * pair + 2, :, :],
+                in_=x_t[:].rearrange("w c u p -> w c p u"),
+            )
+
+        def quantise_x(part):
+            if not 0 <= part < N_PARTS:
+                return
+            x_codes = work.tile([P, R, P], U32, align_bytes=64)
+            x_scales = work.tile([P, R, P], U8, align_bytes=64)
+            nc.vector.quantize_mx(
+                out=x_codes[:].rearrange("w r p -> w (r p)").bitcast(FP8X4),
+                scales=x_scales[:].rearrange("w r p -> w (r p)"),
+                in_=parts[part]["x_grouped"][:],
+            )
+            parts[part]["x_codes"], parts[part]["x_scales"] = x_codes, x_scales
+
+        def project(part):
+            if not 0 <= part < N_PARTS:
+                return
+            v_ps = psum_p.tile([P, R, H], F32, tag="prep")
+            for r in range(R):
+                nc.tensor.matmul_mx(
+                    out=v_ps[:, r, :],
+                    lhsT=parts[part]["x_codes"][:, r, :].bitcast(FP8X4),
+                    lhsT_scale=parts[part]["x_scales"][:, r, :],
+                    rhs=wv_codes[:].bitcast(FP8X4),
+                    rhs_scale=wv_scales[:],
+                    start=True,
+                    stop=True,
+                )
+            parts[part]["v_ps"] = v_ps
+
+        def keep_v(part):
+            if not 0 <= part < N_PARTS:
+                return
+            b, g = divmod(part, J)
+            v_near = seqs[b]["v_near"]
+            nc.scalar.copy(out=v_near[:, g, LW : LW + R, :], in_=parts[part]["v_ps"][:])
+            rows = out[b].rearrange("(m r) h -> m r h", r=R)[:, R - LW : R, :]
+            nc.sync.dma_start(out=rows[g * P : (g + 1) * P], in_=v_near[:, g, R : R + LW, :])
+
+        def fetch_v_before(part):
+            if not 0 <= part < N_PARTS:
+                return
+            b, g = divmod(part, J)
+            v_near = seqs[b]["v_near"]
+            rows = out[b].rearrange("(m r) h -> m r h", r=R)[:, R - LW : R, :]
+            if g == 0:
+                nc.vector.memset(v_near[0:1, 0, 0:LW, :], 0.0)
+                nc.sync.dma_start(out=v_near[1:P, 0, 0:LW, :], in_=rows[0 : P - 1])
+            else:
+                nc.sync.dma_start(out=v_near[:, g, 0:LW, :], in_=rows[g * P - 1 : (g + 1) * P - 1])
+
+        def where(tile):
+            step, j = divmod(tile, J)
+            return step, step // R, R - 1 - step % R, j
+
+        def logits(tile):
+            if not 0 <= tile < N_TILES:
+                return
+            step, b, r, j = where(tile)
+            qk_t = seqs[b]["qk_t"]
+            keys = (j + 1) * P
+            s_ps = psum_s.tile([P, M], F32)
+            nc.tensor.matmul(
+                out=s_ps[:, 0:keys], lhsT=qk_t[:, 0, r, KPAD + j * P : KPAD + keys],
+                rhs=qk_t[:, 1, r, KPAD : KPAD + keys], start=True, stop=False,
+            )
+            if r == 0 and j > 0:
+                nc.tensor.matmul(
+                    out=s_ps[:, 0:P], lhsT=ident_bf[:], rhs=mask_tiles[:, NO_KEY0, :],
+                    start=False, stop=False,
+                )
+            mask_row = CAUSAL_NO_KEY0 if (r == 0 and j == 0) else CAUSAL
+            nc.tensor.matmul(
+                out=s_ps[:, j * P : keys], lhsT=ident_bf[:], rhs=mask_tiles[:, mask_row, :],
+                start=False, stop=True,
+            )
+            logit_tiles[tile] = s_ps
+
+        def far_maximum(tile):
+            if not 0 <= tile < N_TILES:
+                return
+            step, b, r, j = where(tile)
+            if j == 0:
+                steps[step] = dict(
+                    neg_top=small.tile([P, J], F32, name="neg_top"),
+                    e_sums=small.tile([P, J, LW + 1], F32, name="e_sums"),
+                )
+            far_max = small.tile([P, 1], F32)
+            nc.vector.tensor_reduce(
+                out=far_max[:], in_=logit_tiles[tile][:, 0 : (j + 1) * P], axis=AX.X, op=ALU.max
+            )
+            far_maxima[tile] = far_max
+
+        def negated_top(tile):
+            if not 0 <= tile < N_TILES:
+                return
+            step, b, r, j = where(tile)
+            nc.vector.tensor_scalar(
+                out=steps[step]["neg_top"][:, j : j + 1], in0=far_maxima[tile][:], scalar1=-SCALE,
+                scalar2=seqs[b]["near_min"][:, r, j : j + 1], op0=ALU.mult, op1=ALU.min,
+            )
+
+        def exponentials(tile):
+            if not 0 <= tile < N_TILES:
+                return
+            step, b, r, j = where(tile)
+            keys = (j + 1) * P
+            e_sb = work.tile([P, M], BF16, bufs=3)
+            nc.scalar.activation(
+                out=e_sb[:, 0:keys], in_=logit_tiles[tile][:, 0:keys], func=ACT.Exp,
+                bias=steps[step]["neg_top"][:, j : j + 1], scale=SCALE,
+                accum_out=steps[step]["e_sums"][:, j, LW : LW + 1],
+            )
+            e_tiles[tile] = e_sb
+
+        def keys_to_partitions(tile):
+            if not 0 <= tile < N_TILES:
+                return
+            step, b, r, j = where(tile)
+            e_t = psum_e.tile([P, J, P], BF16)
+            for t in range(j + 1):
+                nc.tensor.transpose(e_t[:, t, :], e_tiles[tile][:, t * P : (t + 1) * P], ident_bf[:])
+            nc.scalar.copy(
+                out=e_grouped_pair[step % 2][:, j, :, 0 : j + 1],
+                in_=e_t[:, 0 : j + 1, :].rearrange("p t m -> p m t"),
+            )
+
+        def local_exponentials(step):
+            if not 0 <= step < N_STEPS:
+                return
+            b, r = step // R, R - 1 - step % R
+            exponents = small.tile([P, J, LW], F32)
+            nc.vector.tensor_tensor(
+                out=exponents[:], in0=steps[step]["neg_top"][:].unsqueeze(2).to_broadcast([P, J, LW]),
+                in1=seqs[b]["near"][:, :, r, :].rearrange("p d j -> p j d"), op=ALU.subtract,
+            )
+            nc.scalar.activation(out=steps[step]["e_sums"][:, :, 0:LW], in_=exponents[:], func=ACT.Exp)
+
+        def group_v(step):
+            if not 0 <= step < N_STEPS:
+                return
+            b, r = step // R, R - 1 - step % R
+            v_grouped = work.tile([P, H, PACK], BF16, align_bytes=64)
+            nc.gpsimd.tensor_scalar(
+                out=v_grouped[:], in0=seqs[b]["v_near"][:, :, LW + r, :].rearrange("p t h -> p h t"),
+                scalar1=1.0, scalar2=0.0, op0=ALU.mult, op1=ALU.add,
+            )
+            steps[step]["v_grouped"] = v_grouped
+
+        def denominator(step):
+            if not 0 <= step < N_STEPS:
+                return
+            den = small.tile([P, J], F32)
+            nc.vector.tensor_reduce(out=den[:], in_=steps[step]["e_sums"][:], axis=AX.X, op=ALU.add)
+            steps[step]["den"] = den
+
+        def inverse_denominator(step):
+            if not 0 <= step < N_STEPS:
+                return
+            inv_den = small.tile([P, J], F32)
+            nc.vector.reciprocal(out=inv_den[:], in_=steps[step]["den"][:])
+            steps[step]["inv_den"] = inv_den
+
+        def local_share(step):
+            if not 0 <= step < N_STEPS:
+                return
+            b, r = step // R, R - 1 - step % R
+            e_sums, v_near, inv_den = steps[step]["e_sums"], seqs[b]["v_near"], steps[step]["inv_den"]
+            w_near = small.tile([P, J, LW], F32)
+            nc.vector.tensor_tensor(
+                out=w_near[:], in0=e_sums[:, :, 0:LW],
+                in1=inv_den[:].unsqueeze(2).to_broadcast([P, J, LW]), op=ALU.mult,
+            )
+            share = work.tile([P, J, H], F32)
+            share_2 = work.tile([P, J, H], F32)
+            nc.gpsimd.tensor_tensor(
+                out=share[:], in0=v_near[:, :, LW + r - 1, :],
+                in1=w_near[:, :, 0:1].to_broadcast([P, J, H]), op=ALU.mult,
+            )
+            nc.gpsimd.tensor_tensor(
+                out=share_2[:], in0=v_near[:, :, LW + r - 2, :],
+                in1=w_near[:, :, 1:2].to_broadcast([P, J, H]), op=ALU.mult,
+            )
+            nc.gpsimd.tensor_tensor(out=share[:], in0=share[:], in1=share_2[:], op=ALU.add)
+            steps[step]["share"] = share
+
+        def quantise_e_and_v(step):
+            if not 0 <= step < N_STEPS:
+                return
+            e_codes = work.tile([P, J, P], U32, align_bytes=64)
+            e_scales = work.tile([P, J, P], U8, align_bytes=64)
+            nc.vector.quantize_mx(
+                out=e_codes[:].rearrange("p j m -> p (j m)").bitcast(FP8X4),
+                scales=e_scales[:].rearrange("p j m -> p (j m)"),
+                in_=e_grouped_pair[step % 2][:].rearrange("p j m t -> p (j m t)"),
+            )
+            v_codes = work.tile([P, H], U32, align_bytes=64)
+            v_scales = work.tile([P, H], U8, align_bytes=64)
+            nc.vector.quantize_mx(
+                out=v_codes[:].bitcast(FP8X4), scales=v_scales[:],
+                in_=steps[step]["v_grouped"][:].rearrange("p h t -> p (h t)"),
+            )
+            steps[step]["codes"] = (e_codes, e_scales, v_codes, v_scales)
+
+        def atrous_sum(step):
+            if not 0 <= step < N_STEPS:
+                return
+            e_codes, e_scales, v_codes, v_scales = steps[step]["codes"]
+            o_ps = psum_o.tile([P, J, H], F32)
+            for j in range(J):
+                nc.tensor.matmul_mx(
+                    out=o_ps[:, j, :],
+                    lhsT=e_codes[:, j, :].bitcast(FP8X4),
+                    lhsT_scale=e_scales[:, j, :],
+                    rhs=v_codes[:].bitcast(FP8X4),
+                    rhs_scale=v_scales[:],
+                    start=True,
+                    stop=True,
+                )
+            steps[step]["o_ps"] = o_ps
+
+        def result(step):
+            if not 0 <= step < N_STEPS:
+                return
+            b, r = step // R, R - 1 - step % R
+            o_sb = seqs[b]["o_sb"]
+            for j in range(J):
+                nc.vector.scalar_tensor_tensor(
+                    out=o_sb[:, j, r, :], in0=steps[step]["o_ps"][:, j, :],
+                    scalar=steps[step]["inv_den"][:, j : j + 1], in1=steps[step]["share"][:, j, :],
+                    op0=ALU.mult, op1=ALU.add,
+                )
+            if r == 0:
+                nc.sync.dma_start(out=out[b].rearrange("(j p r) h -> p j r h", j=J, r=R), in_=o_sb[:])
+
+        load(0)
+        for step in range(-R, N_STEPS + 2):
+            part = step + R
+            for j in range(J):
+                tile = step * J + j
+                logits(tile + 3)
+                far_maximum(tile + 3)
+                exponentials(tile + 1)
+                keys_to_partitions(tile)
+                if j == 0:
+                    load(part + 1)
+                    heads_to_partitions(part)
+                    local_logits(part - 1)
+                    quantise_e_and_v(step - 1)
+                    local_minimum(part - 1)
+                if j == 1:
+                    fetch_v_before(part - 2)
+                    x_to_partitions(part, 0)
+                    local_products(part)
+                if j == 2:
+                    atrous_sum(step - 1)
+                    project(part - 1)
+                    x_to_partitions(part, 1)
+                    local_exponentials(step)
+                if j == 3:
+                    local_sums(part)
+                    keep_v(part - 1)
+                    group_v(step)
+                    denominator(step)
+                    quantise_x(part)
+                    inverse_denominator(step)
+                    result(step - 1)
+                    local_share(step)
+                negated_top(tile + 3)

@@ -28,6 +28,8 @@ CAUSAL = 0
 CAUSAL_NO_KEY0 = 1
 NO_KEY0 = 2
 N_MASKS = 3
+ONES = 56
+TILE_ORDER = (2, 0, 1, 3)
 
 N_PARTS = B * J
 N_STEPS = B * R
@@ -69,7 +71,7 @@ def tile_singlehead_pa_t_kernel(tc, q, k_proj, x, Wv, out):
         nc.vector.memset(mask_tiles[:, NO_KEY0, :], 0.0)
         nc.vector.memset(mask_tiles[:, NO_KEY0, 0:1], NEG)
 
-        ones_f32 = const.tile([P, 2], F32)
+        ones_f32 = const.tile([P, ONES], F32)
         nc.vector.memset(ones_f32[:], 1.0)
         no_token = const.tile([P, LW, R, J], F32)
         nc.vector.memset(no_token[:], 0.0)
@@ -146,35 +148,34 @@ def tile_singlehead_pa_t_kernel(tc, q, k_proj, x, Wv, out):
             first = KPAD + g * P
             nc.scalar.copy(out=seqs[b]["qk_t"][:, :, :, first : first + P], in_=heads_t[:])
 
-        def local_products(part):
+        def local_products(part, d):
             if not 0 <= part < N_PARTS:
                 return
             b, g = divmod(part, J)
             qk_t = seqs[b]["qk_t"]
             first = KPAD + g * P
-            products = work.tile([P, LW, R, P], F32)
-            for d in range(1, LW + 1):
-                nc.vector.tensor_tensor(
-                    out=products[:, d - 1, 0:d, :], in0=qk_t[:, 0, 0:d, first : first + P],
-                    in1=qk_t[:, 1, R - d : R, first - 1 : first - 1 + P], op=ALU.mult,
-                )
-                nc.vector.tensor_tensor(
-                    out=products[:, d - 1, d:R, :], in0=qk_t[:, 0, d:R, first : first + P],
-                    in1=qk_t[:, 1, 0 : R - d, first : first + P], op=ALU.mult,
-                )
-            parts[part]["products"] = products
+            if d == 1:
+                parts[part]["products"] = work.tile([P, LW, R, P], F32, name="products")
+            products = parts[part]["products"]
+            nc.vector.tensor_tensor(
+                out=products[:, d - 1, 0:d, :], in0=qk_t[:, 0, 0:d, first : first + P],
+                in1=qk_t[:, 1, R - d : R, first - 1 : first - 1 + P], op=ALU.mult,
+            )
+            nc.vector.tensor_tensor(
+                out=products[:, d - 1, d:R, :], in0=qk_t[:, 0, d:R, first : first + P],
+                in1=qk_t[:, 1, 0 : R - d, first : first + P], op=ALU.mult,
+            )
 
-        def local_sums(part):
+        def local_sums(part, d):
             if not 0 <= part < N_PARTS:
                 return
-            near_ps = psum_p.tile([P, LW, R, 2], F32, tag="prep")
-            for d in range(LW):
-                for r in range(R):
-                    nc.tensor.matmul(
-                        out=near_ps[:, d, r, :], lhsT=parts[part]["products"][:, d, r, :],
-                        rhs=ones_f32[:], start=True, stop=True,
-                    )
-            parts[part]["near_ps"] = near_ps
+            if d == 1:
+                parts[part]["near_ps"] = psum_p.tile([P, LW, R, ONES], F32, tag="prep", name="near_ps")
+            for r in range(R):
+                nc.tensor.matmul(
+                    out=parts[part]["near_ps"][:, d - 1, r, :], lhsT=parts[part]["products"][:, d - 1, r, :],
+                    rhs=ones_f32[:], start=True, stop=True,
+                )
 
         def local_logits(part):
             if not 0 <= part < N_PARTS:
@@ -260,8 +261,8 @@ def tile_singlehead_pa_t_kernel(tc, q, k_proj, x, Wv, out):
                 nc.sync.dma_start(out=v_near[:, g, 0:LW, :], in_=rows[g * P - 1 : (g + 1) * P - 1])
 
         def where(tile):
-            step, j = divmod(tile, J)
-            return step, step // R, R - 1 - step % R, j
+            step, turn = divmod(tile, J)
+            return step, step // R, R - 1 - step % R, TILE_ORDER[turn]
 
         def logits(tile):
             if not 0 <= tile < N_TILES:
@@ -290,7 +291,7 @@ def tile_singlehead_pa_t_kernel(tc, q, k_proj, x, Wv, out):
             if not 0 <= tile < N_TILES:
                 return
             step, b, r, j = where(tile)
-            if j == 0:
+            if tile % J == 0:
                 steps[step] = dict(
                     neg_top=small.tile([P, J], F32, name="neg_top"),
                     e_sums=small.tile([P, J, LW + 1], F32, name="e_sums"),
@@ -351,9 +352,8 @@ def tile_singlehead_pa_t_kernel(tc, q, k_proj, x, Wv, out):
                 return
             b, r = step // R, R - 1 - step % R
             v_grouped = work.tile([P, H, PACK], BF16, align_bytes=64)
-            nc.gpsimd.tensor_scalar(
-                out=v_grouped[:], in0=seqs[b]["v_near"][:, :, LW + r, :].rearrange("p t h -> p h t"),
-                scalar1=1.0, scalar2=0.0, op0=ALU.mult, op1=ALU.add,
+            nc.scalar.copy(
+                out=v_grouped[:], in_=seqs[b]["v_near"][:, :, LW + r, :].rearrange("p t h -> p h t")
             )
             steps[step]["v_grouped"] = v_grouped
 
@@ -371,28 +371,17 @@ def tile_singlehead_pa_t_kernel(tc, q, k_proj, x, Wv, out):
             nc.vector.reciprocal(out=inv_den[:], in_=steps[step]["den"][:])
             steps[step]["inv_den"] = inv_den
 
-        def local_share(step):
+        def local_weights(step):
             if not 0 <= step < N_STEPS:
                 return
             b, r = step // R, R - 1 - step % R
-            e_sums, v_near, inv_den = steps[step]["e_sums"], seqs[b]["v_near"], steps[step]["inv_den"]
+            e_sums, inv_den = steps[step]["e_sums"], steps[step]["inv_den"]
             w_near = small.tile([P, J, LW], F32)
             nc.vector.tensor_tensor(
                 out=w_near[:], in0=e_sums[:, :, 0:LW],
                 in1=inv_den[:].unsqueeze(2).to_broadcast([P, J, LW]), op=ALU.mult,
             )
-            share = work.tile([P, J, H], F32)
-            share_2 = work.tile([P, J, H], F32)
-            nc.gpsimd.tensor_tensor(
-                out=share[:], in0=v_near[:, :, LW + r - 1, :],
-                in1=w_near[:, :, 0:1].to_broadcast([P, J, H]), op=ALU.mult,
-            )
-            nc.gpsimd.tensor_tensor(
-                out=share_2[:], in0=v_near[:, :, LW + r - 2, :],
-                in1=w_near[:, :, 1:2].to_broadcast([P, J, H]), op=ALU.mult,
-            )
-            nc.gpsimd.tensor_tensor(out=share[:], in0=share[:], in1=share_2[:], op=ALU.add)
-            steps[step]["share"] = share
+            steps[step]["w_near"] = w_near
 
         def quantise_e_and_v(step):
             if not 0 <= step < N_STEPS:
@@ -429,15 +418,34 @@ def tile_singlehead_pa_t_kernel(tc, q, k_proj, x, Wv, out):
                 )
             steps[step]["o_ps"] = o_ps
 
+        def local_share(step, d):
+            if not 0 <= step < N_STEPS:
+                return
+            b, r = step // R, R - 1 - step % R
+            v_near, w_near = seqs[b]["v_near"], steps[step]["w_near"]
+            if d == LW:
+                steps[step]["share"] = work.tile([P, J, H], F32, name="share")
+            share = steps[step]["share"]
+            for j in range(J):
+                if d == LW:
+                    nc.vector.tensor_scalar_mul(
+                        out=share[:, j, :], in0=v_near[:, j, LW + r - d, :], scalar1=w_near[:, j, d - 1 : d]
+                    )
+                else:
+                    nc.vector.scalar_tensor_tensor(
+                        out=share[:, j, :], in0=v_near[:, j, LW + r - d, :], scalar=w_near[:, j, d - 1 : d],
+                        in1=share[:, j, :], op0=ALU.mult, op1=ALU.add,
+                    )
+
         def result(step):
             if not 0 <= step < N_STEPS:
                 return
             b, r = step // R, R - 1 - step % R
-            o_sb = seqs[b]["o_sb"]
+            o_sb, share = seqs[b]["o_sb"], steps[step]["share"]
             for j in range(J):
                 nc.vector.scalar_tensor_tensor(
                     out=o_sb[:, j, r, :], in0=steps[step]["o_ps"][:, j, :],
-                    scalar=steps[step]["inv_den"][:, j : j + 1], in1=steps[step]["share"][:, j, :],
+                    scalar=steps[step]["inv_den"][:, j : j + 1], in1=share[:, j, :],
                     op0=ALU.mult, op1=ALU.add,
                 )
             if r == 0:
@@ -448,6 +456,8 @@ def tile_singlehead_pa_t_kernel(tc, q, k_proj, x, Wv, out):
             part = step + R
             for j in range(J):
                 tile = step * J + j
+                if j == 0:
+                    local_logits(part - 1)
                 logits(tile + 3)
                 far_maximum(tile + 3)
                 exponentials(tile + 1)
@@ -455,25 +465,31 @@ def tile_singlehead_pa_t_kernel(tc, q, k_proj, x, Wv, out):
                 if j == 0:
                     load(part + 1)
                     heads_to_partitions(part)
-                    local_logits(part - 1)
+                    x_to_partitions(part, 0)
                     quantise_e_and_v(step - 1)
                     local_minimum(part - 1)
+                    negated_top(tile + 3)
+                    inverse_denominator(step - 1)
                 if j == 1:
                     fetch_v_before(part - 2)
-                    x_to_partitions(part, 0)
-                    local_products(part)
+                    project(part - 1)
+                    keep_v(part - 1)
+                    local_products(part, 1)
+                    negated_top(tile + 3)
+                    local_weights(step - 1)
+                    local_products(part, 2)
                 if j == 2:
                     atrous_sum(step - 1)
-                    project(part - 1)
                     x_to_partitions(part, 1)
+                    local_sums(part, 1)
+                    local_share(step - 1, 2)
+                    negated_top(tile + 3)
                     local_exponentials(step)
+                    local_share(step - 1, 1)
                 if j == 3:
-                    local_sums(part)
-                    keep_v(part - 1)
+                    local_sums(part, 2)
                     group_v(step)
-                    denominator(step)
                     quantise_x(part)
-                    inverse_denominator(step)
+                    negated_top(tile + 3)
+                    denominator(step)
                     result(step - 1)
-                    local_share(step)
-                negated_top(tile + 3)

@@ -23,12 +23,21 @@ J = M // P
 SCALE = 1.0 / math.sqrt(D)
 NEG = -1.0e30
 KPAD = 16
+KROW = KPAD + M
+
+GROUP = 32
+GROUPS = P // GROUP
+ZSTEP = P + GROUP
+ZROW = GROUPS * ZSTEP
+KEY_ROWS = (2, 3, 0, 1)
 
 CAUSAL = 0
 CAUSAL_NO_KEY0 = 1
-NO_KEY0 = 2
-N_MASKS = 3
-ONES = 56
+N_MASKS = 2
+OWN_COLUMN = 0
+FIRST_TOKENS = 1
+N_NEAR_MASKS = 2
+KEY0_COLS = 2
 TILE_ORDER = (2, 0, 1, 3)
 
 N_PARTS = B * J
@@ -61,22 +70,27 @@ def tile_singlehead_pa_t_kernel(tc, q, k_proj, x, Wv, out):
         nc.gpsimd.memset(causal_f32[:], 0.0)
         nc.gpsimd.affine_select(
             out=causal_f32[:], in_=causal_f32[:], compare_op=ALU.is_ge, fill=NEG,
-            base=0, pattern=[[-1, P]], channel_multiplier=1,
+            base=0, pattern=[[1, P]], channel_multiplier=-1,
         )
-        mask_tiles = const.tile([P, N_MASKS, P], BF16)
+        mask_tiles = const.tile([P, N_MASKS, P], F32)
         nc.vector.tensor_copy(out=mask_tiles[:, CAUSAL, :], in_=causal_f32[:])
         nc.vector.tensor_copy(out=mask_tiles[:, CAUSAL_NO_KEY0, :], in_=causal_f32[:])
-        nc.vector.memset(mask_tiles[:, CAUSAL_NO_KEY0, 0:1], NEG)
-        nc.vector.memset(mask_tiles[0:1, CAUSAL_NO_KEY0, 0:1], 0.0)
-        nc.vector.memset(mask_tiles[:, NO_KEY0, :], 0.0)
-        nc.vector.memset(mask_tiles[:, NO_KEY0, 0:1], NEG)
+        nc.vector.memset(mask_tiles[0:1, CAUSAL_NO_KEY0, 1:P], NEG)
+        no_key0 = const.tile([P, KEY0_COLS], BF16)
+        nc.vector.memset(no_key0[:], 0.0)
+        nc.vector.memset(no_key0[:, 0:1], NEG)
 
-        ones_f32 = const.tile([P, ONES], F32)
-        nc.vector.memset(ones_f32[:], 1.0)
-        no_token = const.tile([P, LW, R, J], F32)
-        nc.vector.memset(no_token[:], 0.0)
-        for d in range(1, LW + 1):
-            nc.vector.memset(no_token[0:1, d - 1, 0:d, 0:1], -SCALE * NEG)
+        same_column = const.tile([P, GROUP], F32)
+        nc.vector.tensor_reduce(
+            out=same_column[:], in_=ident_f32[:].rearrange("p (a c) -> p c a", c=GROUP), axis=AX.X, op=ALU.add
+        )
+        near_masks = const.tile([P, N_NEAR_MASKS, GROUPS, GROUP], F32)
+        for row in range(N_NEAR_MASKS):
+            nc.vector.tensor_scalar(
+                out=near_masks[:, row], in0=same_column[:].unsqueeze(1).to_broadcast([P, GROUPS, GROUP]),
+                scalar1=-1.0, scalar2=-NEG, op0=ALU.add, op1=ALU.mult,
+            )
+        nc.vector.memset(near_masks[0 : 3 * GROUP, FIRST_TOKENS, 0, 0:1], NEG)
 
         e_grouped_pair = [
             const.tile([P, J, P, PACK], BF16, align_bytes=64, name="e_grouped_0"),
@@ -86,11 +100,17 @@ def tile_singlehead_pa_t_kernel(tc, q, k_proj, x, Wv, out):
             nc.vector.memset(e_grouped[:], 0.0)
 
         qk_t_pair = [
-            const.tile([P, 2, R, KPAD + M], BF16, name="qk_t_0"),
-            const.tile([P, 2, R, KPAD + M], BF16, name="qk_t_1"),
+            const.tile([P, 2, R, KROW], BF16, name="qk_t_0"),
+            const.tile([P, 2, R, KROW], BF16, name="qk_t_1"),
         ]
         for qk_t in qk_t_pair:
             nc.vector.memset(qk_t[:, 1, :, 0:KPAD], 0.0)
+        q_groups_pair = [
+            const.tile([P, R, ZROW], BF16, name="q_groups_0"),
+            const.tile([P, R, ZROW], BF16, name="q_groups_1"),
+        ]
+        for q_groups in q_groups_pair:
+            nc.vector.memset(q_groups[:], 0.0)
 
         def transpose_words(words_out, words_in):
             for u in range(2):
@@ -142,49 +162,70 @@ def tile_singlehead_pa_t_kernel(tc, q, k_proj, x, Wv, out):
                 )
             qk_in = parts[part]["qk_in"]
             heads_t = psum_p.tile([P, 2, R, P], BF16, tag="prep")
-            for side in range(2):
-                for r in range(R):
-                    nc.tensor.transpose(heads_t[:, side, r, :], qk_in[:, side, r, :], ident_bf[:])
+            for r in range(R):
+                nc.tensor.transpose(heads_t[:, 0, r, :], qk_in[:, 0, r, :], ident_bf[:])
+            for row in range(R):
+                nc.tensor.transpose(heads_t[:, 1, row, :], qk_in[:, 1, KEY_ROWS[row], :], ident_bf[:])
             first = KPAD + g * P
             nc.scalar.copy(out=seqs[b]["qk_t"][:, :, :, first : first + P], in_=heads_t[:])
 
-        def local_products(part, d):
+        def group_queries(part):
             if not 0 <= part < N_PARTS:
                 return
             b, g = divmod(part, J)
-            qk_t = seqs[b]["qk_t"]
             first = KPAD + g * P
-            if d == 1:
-                parts[part]["products"] = work.tile([P, LW, R, P], F32, name="products")
-            products = parts[part]["products"]
-            nc.vector.tensor_tensor(
-                out=products[:, d - 1, 0:d, :], in0=qk_t[:, 0, 0:d, first : first + P],
-                in1=qk_t[:, 1, R - d : R, first - 1 : first - 1 + P], op=ALU.mult,
-            )
-            nc.vector.tensor_tensor(
-                out=products[:, d - 1, d:R, :], in0=qk_t[:, 0, d:R, first : first + P],
-                in1=qk_t[:, 1, 0 : R - d, first : first + P], op=ALU.mult,
+            nc.vector.tensor_copy(
+                out=q_groups_pair[part % 2][:].rearrange("h r (gg s) -> h r gg s", s=ZSTEP)[:, :, :, 0:GROUP],
+                in_=seqs[b]["qk_t"][:, 0, :, first : first + P].rearrange("h r (gg c) -> h r gg c", c=GROUP),
             )
 
-        def local_sums(part, d):
+        def local_keys(keys, r, column):
+            if r == 0:
+                return keys[:, 0:2, column - 1 : column - 1 + GROUP]
+            if r == 1:
+                step = KROW + 1
+                first = KROW + column - 1
+                flat = keys.rearrange("h row c -> h (row c)")[:, first : first + 2 * step]
+                return flat.rearrange("h (d c) -> h d c", d=2)[:, :, 0:GROUP]
+            if r == 2:
+                return keys[:, 2:4, column : column + GROUP]
+            return keys[:, 0:4:3, column : column + GROUP]
+
+        def local_dots(part, pair):
             if not 0 <= part < N_PARTS:
                 return
-            if d == 1:
-                parts[part]["near_ps"] = psum_p.tile([P, LW, R, ONES], F32, tag="prep", name="near_ps")
-            for r in range(R):
-                nc.tensor.matmul(
-                    out=parts[part]["near_ps"][:, d - 1, r, :], lhsT=parts[part]["products"][:, d - 1, r, :],
-                    rhs=ones_f32[:], start=True, stop=True,
-                )
+            b, g = divmod(part, J)
+            if pair == 0:
+                parts[part]["near_ps"] = psum_p.tile([P, R, LW, GROUP], F32, tag="prep", name="near_ps")
+            near_ps = parts[part]["near_ps"]
+            row = FIRST_TOKENS if (g == 0 and pair == 0) else OWN_COLUMN
+            nc.tensor.matmul(
+                out=near_ps[:, 2 * pair : 2 * pair + 2].rearrange("p r d c -> p (r d c)"),
+                lhsT=near_masks[:, row].rearrange("p gg c -> p (gg c)"), rhs=ident_f32[:],
+                is_transpose=True, start=True, stop=False,
+            )
+            for r in (2 * pair, 2 * pair + 1):
+                for gg in range(GROUPS):
+                    nc.tensor.matmul(
+                        out=near_ps[:, r], lhsT=q_groups_pair[part % 2][:, r, gg * P : (gg + 1) * P],
+                        rhs=local_keys(seqs[b]["qk_t"][:, 1], r, KPAD + g * P + gg * GROUP),
+                        start=False, stop=(r == 2 * pair + 1 and gg == GROUPS - 1),
+                    )
+
+        def own_columns(part):
+            if not 0 <= part < N_PARTS:
+                return
+            near_raw = small.tile([P, R, LW], F32)
+            nc.vector.tensor_reduce(out=near_raw[:], in_=parts[part]["near_ps"][:], axis=AX.X, op=ALU.max)
+            parts[part]["near_raw"] = near_raw
 
         def local_logits(part):
             if not 0 <= part < N_PARTS:
                 return
             b, g = divmod(part, J)
-            near = seqs[b]["near"]
-            nc.vector.scalar_tensor_tensor(
-                out=near[:, :, :, g], in0=parts[part]["near_ps"][:, :, :, 0], scalar=-SCALE,
-                in1=no_token[:, :, :, g], op0=ALU.mult, op1=ALU.add,
+            nc.vector.tensor_scalar_mul(
+                out=seqs[b]["near"][:, :, :, g], in0=parts[part]["near_raw"][:].rearrange("p r d -> p d r"),
+                scalar1=-SCALE,
             )
 
         def local_minimum(part):
@@ -273,17 +314,16 @@ def tile_singlehead_pa_t_kernel(tc, q, k_proj, x, Wv, out):
             s_ps = psum_s.tile([P, M], F32)
             nc.tensor.matmul(
                 out=s_ps[:, 0:keys], lhsT=qk_t[:, 0, r, KPAD + j * P : KPAD + keys],
-                rhs=qk_t[:, 1, r, KPAD : KPAD + keys], start=True, stop=False,
+                rhs=qk_t[:, 1, KEY_ROWS.index(r), KPAD : KPAD + keys], start=True, stop=False,
             )
             if r == 0 and j > 0:
                 nc.tensor.matmul(
-                    out=s_ps[:, 0:P], lhsT=ident_bf[:], rhs=mask_tiles[:, NO_KEY0, :],
-                    start=False, stop=False,
+                    out=s_ps[:, 0:KEY0_COLS], lhsT=ident_bf[:], rhs=no_key0[:], start=False, stop=False,
                 )
             mask_row = CAUSAL_NO_KEY0 if (r == 0 and j == 0) else CAUSAL
             nc.tensor.matmul(
-                out=s_ps[:, j * P : keys], lhsT=ident_bf[:], rhs=mask_tiles[:, mask_row, :],
-                start=False, stop=True,
+                out=s_ps[:, j * P : keys], lhsT=mask_tiles[:, mask_row, :], rhs=ident_f32[:],
+                is_transpose=True, start=False, stop=True,
             )
             logit_tiles[tile] = s_ps
 
@@ -423,17 +463,18 @@ def tile_singlehead_pa_t_kernel(tc, q, k_proj, x, Wv, out):
                 return
             b, r = step // R, R - 1 - step % R
             v_near, w_near = seqs[b]["v_near"], steps[step]["w_near"]
+            place = d - 1 if r == R - 1 else LW - d
             if d == LW:
                 steps[step]["share"] = work.tile([P, J, H], F32, name="share")
             share = steps[step]["share"]
             for j in range(J):
                 if d == LW:
                     nc.vector.tensor_scalar_mul(
-                        out=share[:, j, :], in0=v_near[:, j, LW + r - d, :], scalar1=w_near[:, j, d - 1 : d]
+                        out=share[:, j, :], in0=v_near[:, j, LW + r - d, :], scalar1=w_near[:, j, place : place + 1]
                     )
                 else:
                     nc.vector.scalar_tensor_tensor(
-                        out=share[:, j, :], in0=v_near[:, j, LW + r - d, :], scalar=w_near[:, j, d - 1 : d],
+                        out=share[:, j, :], in0=v_near[:, j, LW + r - d, :], scalar=w_near[:, j, place : place + 1],
                         in1=share[:, j, :], op0=ALU.mult, op1=ALU.add,
                     )
 
@@ -457,7 +498,7 @@ def tile_singlehead_pa_t_kernel(tc, q, k_proj, x, Wv, out):
             for j in range(J):
                 tile = step * J + j
                 if j == 0:
-                    local_logits(part - 1)
+                    own_columns(part - 1)
                 logits(tile + 3)
                 far_maximum(tile + 3)
                 exponentials(tile + 1)
@@ -466,6 +507,7 @@ def tile_singlehead_pa_t_kernel(tc, q, k_proj, x, Wv, out):
                     load(part + 1)
                     heads_to_partitions(part)
                     x_to_partitions(part, 0)
+                    local_logits(part - 1)
                     quantise_e_and_v(step - 1)
                     local_minimum(part - 1)
                     negated_top(tile + 3)
@@ -474,20 +516,19 @@ def tile_singlehead_pa_t_kernel(tc, q, k_proj, x, Wv, out):
                     fetch_v_before(part - 2)
                     project(part - 1)
                     keep_v(part - 1)
-                    local_products(part, 1)
+                    group_queries(part)
                     negated_top(tile + 3)
                     local_weights(step - 1)
-                    local_products(part, 2)
                 if j == 2:
                     atrous_sum(step - 1)
                     x_to_partitions(part, 1)
-                    local_sums(part, 1)
+                    local_dots(part, 0)
                     local_share(step - 1, 2)
                     negated_top(tile + 3)
                     local_exponentials(step)
                     local_share(step - 1, 1)
                 if j == 3:
-                    local_sums(part, 2)
+                    local_dots(part, 1)
                     group_v(step)
                     quantise_x(part)
                     negated_top(tile + 3)

@@ -57,7 +57,7 @@ def tile_singlehead_pa_t_kernel(tc, q, k_proj, x, Wv, out):
         work = ctx.enter_context(tc.tile_pool(name="work", bufs=2))
         small = ctx.enter_context(tc.tile_pool(name="small", bufs=4))
         psum_s = ctx.enter_context(tc.psum_pool(name="psum_s", bufs=3))
-        psum_e = ctx.enter_context(tc.psum_pool(name="psum_e", bufs=2))
+        psum_e = ctx.enter_context(tc.psum_pool(name="psum_e", bufs=1))
         psum_o = ctx.enter_context(tc.psum_pool(name="psum_o", bufs=1))
         psum_p = ctx.enter_context(tc.psum_pool(name="psum_p", bufs=2))
 
@@ -92,13 +92,6 @@ def tile_singlehead_pa_t_kernel(tc, q, k_proj, x, Wv, out):
             )
         nc.vector.memset(near_masks[0 : 3 * GROUP, FIRST_TOKENS, 0, 0:1], NEG)
 
-        e_grouped_pair = [
-            const.tile([P, J, P, PACK], BF16, align_bytes=64, name="e_grouped_0"),
-            const.tile([P, J, P, PACK], BF16, align_bytes=64, name="e_grouped_1"),
-        ]
-        for e_grouped in e_grouped_pair:
-            nc.vector.memset(e_grouped[:], 0.0)
-
         qk_t_pair = [
             const.tile([P, 2, R, KROW], BF16, name="qk_t_0"),
             const.tile([P, 2, R, KROW], BF16, name="qk_t_1"),
@@ -110,7 +103,7 @@ def tile_singlehead_pa_t_kernel(tc, q, k_proj, x, Wv, out):
             const.tile([P, R, ZROW], BF16, name="q_groups_1"),
         ]
         for q_groups in q_groups_pair:
-            nc.vector.memset(q_groups[:], 0.0)
+            nc.gpsimd.memset(q_groups[:].rearrange("h r c -> h (r c)").bitcast(F32), 0.0)
 
         def transpose_words(words_out, words_in):
             for u in range(2):
@@ -129,12 +122,29 @@ def tile_singlehead_pa_t_kernel(tc, q, k_proj, x, Wv, out):
         wv_scales = const.tile([P, H], U8, align_bytes=64)
         nc.vector.quantize_mx(out=wv_codes[:].bitcast(FP8X4), scales=wv_scales[:], in_=wv_grouped[:])
 
+        e_rows_pair = [
+            [const.tile([P, (j // 2 + 1) * 2 * P], BF16, name="e_rows_%d_%d" % (side, j)) for j in range(J)]
+            for side in range(2)
+        ]
+        for e_rows in e_rows_pair:
+            for j in range(0, J, 2):
+                nc.vector.memset(e_rows[j][:, j * P :], 0.0)
+        e_sums_pair = [
+            const.tile([P, J, LW + 2], F32, name="e_sums_0"),
+            const.tile([P, J, LW + 2], F32, name="e_sums_1"),
+        ]
+        for e_sums in e_sums_pair:
+            nc.vector.memset(e_sums[:], 0.0)
+        e_words_t = [psum_e.tile([P, 2, 2, P], F32, name="e_words_t_%d" % half) for half in range(2)]
+        zeros_f32 = const.tile([P, P], F32)
+        nc.vector.memset(zeros_f32[:], 0.0)
+        for odd in range(2):
+            nc.tensor.transpose(e_words_t[0][:, odd, 1, :], zeros_f32[:], ident_f32[:])
+
         seqs = {}
         parts = {}
         steps = {}
         logit_tiles = {}
-        far_maxima = {}
-        e_tiles = {}
 
         def load(part):
             if not 0 <= part < N_PARTS:
@@ -327,53 +337,58 @@ def tile_singlehead_pa_t_kernel(tc, q, k_proj, x, Wv, out):
             )
             logit_tiles[tile] = s_ps
 
-        def far_maximum(tile):
+        def negated_top(tile):
             if not 0 <= tile < N_TILES:
                 return
             step, b, r, j = where(tile)
             if tile % J == 0:
                 steps[step] = dict(
                     neg_top=small.tile([P, J], F32, name="neg_top"),
-                    e_sums=small.tile([P, J, LW + 1], F32, name="e_sums"),
+                    e_sums=e_sums_pair[step % 2],
+                    e_grouped=work.tile([P, J, P, PACK], BF16, align_bytes=64, name="e_grouped"),
                 )
-            far_max = small.tile([P, 1], F32)
-            nc.vector.tensor_reduce(
-                out=far_max[:], in_=logit_tiles[tile][:, 0 : (j + 1) * P], axis=AX.X, op=ALU.max
-            )
-            far_maxima[tile] = far_max
-
-        def negated_top(tile):
-            if not 0 <= tile < N_TILES:
-                return
-            step, b, r, j = where(tile)
+            minus_s = work.tile([P, M], BF16)
             nc.vector.tensor_scalar(
-                out=steps[step]["neg_top"][:, j : j + 1], in0=far_maxima[tile][:], scalar1=-SCALE,
+                out=minus_s[:, 0 : (j + 1) * P], in0=logit_tiles[tile][:, 0 : (j + 1) * P], scalar1=-SCALE,
                 scalar2=seqs[b]["near_min"][:, r, j : j + 1], op0=ALU.mult, op1=ALU.min,
+                accum_out=steps[step]["neg_top"][:, j : j + 1],
             )
 
         def exponentials(tile):
             if not 0 <= tile < N_TILES:
                 return
             step, b, r, j = where(tile)
-            keys = (j + 1) * P
-            e_sb = work.tile([P, M], BF16, bufs=3)
-            nc.scalar.activation(
-                out=e_sb[:, 0:keys], in_=logit_tiles[tile][:, 0:keys], func=ACT.Exp,
-                bias=steps[step]["neg_top"][:, j : j + 1], scale=SCALE,
-                accum_out=steps[step]["e_sums"][:, j, LW : LW + 1],
-            )
-            e_tiles[tile] = e_sb
+            e_rows = e_rows_pair[step % 2][j]
+            pairs = (j + 1) // 2 * 2 * P
+            neg_top = steps[step]["neg_top"][:, j : j + 1]
+            if pairs > 0:
+                nc.scalar.activation(
+                    out=e_rows[:, 0:pairs].rearrange("p (u w e) -> p u w e", e=2, w=P),
+                    in_=logit_tiles[tile][:, 0:pairs].rearrange("p (u e w) -> p u w e", e=2, w=P),
+                    func=ACT.Exp, bias=neg_top, scale=SCALE,
+                    accum_out=steps[step]["e_sums"][:, j, LW : LW + 1],
+                )
+            if j % 2 == 0:
+                column = LW + (1 if pairs > 0 else 0)
+                nc.scalar.activation(
+                    out=e_rows[:, pairs:].rearrange("p (w e) -> p w e", e=2)[:, :, 0],
+                    in_=logit_tiles[tile][:, pairs : pairs + P],
+                    func=ACT.Exp, bias=neg_top, scale=SCALE,
+                    accum_out=steps[step]["e_sums"][:, j, column : column + 1],
+                )
 
         def keys_to_partitions(tile):
             if not 0 <= tile < N_TILES:
                 return
             step, b, r, j = where(tile)
-            e_t = psum_e.tile([P, J, P], BF16)
-            for t in range(j + 1):
-                nc.tensor.transpose(e_t[:, t, :], e_tiles[tile][:, t * P : (t + 1) * P], ident_bf[:])
+            words = e_rows_pair[step % 2][j][:].bitcast(F32)
+            words_t = e_words_t[j // 2][:, j % 2]
+            for u in range(j // 2 + 1):
+                nc.tensor.transpose(words_t[:, u, :], words[:, u * P : (u + 1) * P], ident_f32[:])
             nc.scalar.copy(
-                out=e_grouped_pair[step % 2][:, j, :, 0 : j + 1],
-                in_=e_t[:, 0 : j + 1, :].rearrange("p t m -> p m t"),
+                out=steps[step]["e_grouped"][:, j].rearrange("p m t -> p (m t)").bitcast(F32).rearrange(
+                    "p (m u) -> p m u", u=2),
+                in_=words_t.rearrange("p u m -> p m u"),
             )
 
         def local_exponentials(step):
@@ -431,7 +446,7 @@ def tile_singlehead_pa_t_kernel(tc, q, k_proj, x, Wv, out):
             nc.vector.quantize_mx(
                 out=e_codes[:].rearrange("p j m -> p (j m)").bitcast(FP8X4),
                 scales=e_scales[:].rearrange("p j m -> p (j m)"),
-                in_=e_grouped_pair[step % 2][:].rearrange("p j m t -> p (j m t)"),
+                in_=steps[step]["e_grouped"][:].rearrange("p j m t -> p (j m t)"),
             )
             v_codes = work.tile([P, H], U32, align_bytes=64)
             v_scales = work.tile([P, H], U8, align_bytes=64)
@@ -498,39 +513,35 @@ def tile_singlehead_pa_t_kernel(tc, q, k_proj, x, Wv, out):
             for j in range(J):
                 tile = step * J + j
                 if j == 0:
-                    own_columns(part - 1)
+                    local_minimum(part - 1)
                 logits(tile + 3)
-                far_maximum(tile + 3)
+                negated_top(tile + 3)
                 exponentials(tile + 1)
                 keys_to_partitions(tile)
                 if j == 0:
                     load(part + 1)
                     heads_to_partitions(part)
                     x_to_partitions(part, 0)
-                    local_logits(part - 1)
                     quantise_e_and_v(step - 1)
-                    local_minimum(part - 1)
-                    negated_top(tile + 3)
                     inverse_denominator(step - 1)
                 if j == 1:
                     fetch_v_before(part - 2)
                     project(part - 1)
                     keep_v(part - 1)
                     group_queries(part)
-                    negated_top(tile + 3)
                     local_weights(step - 1)
                 if j == 2:
                     atrous_sum(step - 1)
                     x_to_partitions(part, 1)
                     local_dots(part, 0)
+                    local_dots(part, 1)
                     local_share(step - 1, 2)
-                    negated_top(tile + 3)
                     local_exponentials(step)
                     local_share(step - 1, 1)
                 if j == 3:
-                    local_dots(part, 1)
+                    own_columns(part)
                     group_v(step)
                     quantise_x(part)
-                    negated_top(tile + 3)
+                    local_logits(part)
                     denominator(step)
                     result(step - 1)

@@ -38,7 +38,9 @@ OWN_COLUMN = 0
 FIRST_TOKENS = 1
 N_NEAR_MASKS = 2
 KEY0_COLS = 2
-TILE_ORDER = (2, 0, 1, 3)
+TILE_ORDER = (0, 2, 1, 3)
+
+FILL, FILL_ALONE = 1024, 768
 
 N_PARTS = B * J
 N_STEPS = B * R
@@ -56,7 +58,7 @@ def tile_singlehead_pa_t_kernel(tc, q, k_proj, x, Wv, out):
         whole = ctx.enter_context(tc.tile_pool(name="whole", bufs=2))
         work = ctx.enter_context(tc.tile_pool(name="work", bufs=2))
         small = ctx.enter_context(tc.tile_pool(name="small", bufs=4))
-        psum_s = ctx.enter_context(tc.psum_pool(name="psum_s", bufs=3))
+        psum_s = ctx.enter_context(tc.psum_pool(name="psum_s", bufs=1))
         psum_e = ctx.enter_context(tc.psum_pool(name="psum_e", bufs=1))
         psum_o = ctx.enter_context(tc.psum_pool(name="psum_o", bufs=1))
         psum_p = ctx.enter_context(tc.psum_pool(name="psum_p", bufs=2))
@@ -141,12 +143,14 @@ def tile_singlehead_pa_t_kernel(tc, q, k_proj, x, Wv, out):
         for odd in range(2):
             nc.tensor.transpose(e_words_t[0][:, odd, 1, :], zeros_f32[:], ident_f32[:])
 
+        banks = [psum_s.tile([P, M], F32, name="logits_%d" % n) for n in range(3)]
+        logit_places = [banks[0][:, 0:P], banks[1][:, 0 : 2 * P], banks[0][:, P:M], banks[2][:]]
+        near_ps = banks[1][:, 2 * P : M].rearrange("p (r d c) -> p r d c", r=R, d=LW)
         seqs = {}
         parts = {}
         steps = {}
-        logit_tiles = {}
 
-        def load(part):
+        def load_qk(part):
             if not 0 <= part < N_PARTS:
                 return
             b, g = divmod(part, J)
@@ -154,9 +158,16 @@ def tile_singlehead_pa_t_kernel(tc, q, k_proj, x, Wv, out):
             qk_in = loads.tile([P, 2, R, H], BF16)
             nc.sync.dma_start(out=qk_in[:, 0], in_=q[b, tokens, :].rearrange("(p r) h -> p r h", r=R))
             nc.sync.dma_start(out=qk_in[:, 1], in_=k_proj[b, tokens, :].rearrange("(p r) h -> p r h", r=R))
+            parts[part] = dict(qk_in=qk_in)
+
+        def load_x(part):
+            if not 0 <= part < N_PARTS:
+                return
+            b, g = divmod(part, J)
+            tokens = slice(g * R * P, (g + 1) * R * P)
             x_in = loads.tile([P, R * D], BF16)
             nc.sync.dma_start(out=x_in[:], in_=x[b, tokens, :].rearrange("(p r) d -> p (r d)", r=R))
-            parts[part] = dict(qk_in=qk_in, x_in=x_in)
+            parts[part]["x_in"] = x_in
 
         def heads_to_partitions(part):
             if not 0 <= part < N_PARTS:
@@ -165,7 +176,7 @@ def tile_singlehead_pa_t_kernel(tc, q, k_proj, x, Wv, out):
             if g == 0:
                 seqs[b] = dict(
                     qk_t=qk_t_pair[b % 2],
-                    v_near=whole.tile([P, J, LW + R, H], F32, name="v_near"),
+                    v_near=whole.tile([P, J, LW + R, H], F32, bufs=3, name="v_near"),
                     near=whole.tile([P, LW, R, J], F32, name="near"),
                     near_min=whole.tile([P, R, J], F32, name="near_min"),
                     o_sb=whole.tile([P, J, R, H], F32, name="o_sb"),
@@ -205,9 +216,6 @@ def tile_singlehead_pa_t_kernel(tc, q, k_proj, x, Wv, out):
             if not 0 <= part < N_PARTS:
                 return
             b, g = divmod(part, J)
-            if pair == 0:
-                parts[part]["near_ps"] = psum_p.tile([P, R, LW, GROUP], F32, tag="prep", name="near_ps")
-            near_ps = parts[part]["near_ps"]
             row = FIRST_TOKENS if (g == 0 and pair == 0) else OWN_COLUMN
             nc.tensor.matmul(
                 out=near_ps[:, 2 * pair : 2 * pair + 2].rearrange("p r d c -> p (r d c)"),
@@ -226,7 +234,7 @@ def tile_singlehead_pa_t_kernel(tc, q, k_proj, x, Wv, out):
             if not 0 <= part < N_PARTS:
                 return
             near_raw = small.tile([P, R, LW], F32)
-            nc.vector.tensor_reduce(out=near_raw[:], in_=parts[part]["near_ps"][:], axis=AX.X, op=ALU.max)
+            nc.vector.tensor_reduce(out=near_raw[:], in_=near_ps, axis=AX.X, op=ALU.max)
             parts[part]["near_raw"] = near_raw
 
         def local_logits(part):
@@ -296,6 +304,12 @@ def tile_singlehead_pa_t_kernel(tc, q, k_proj, x, Wv, out):
             b, g = divmod(part, J)
             v_near = seqs[b]["v_near"]
             nc.scalar.copy(out=v_near[:, g, LW : LW + R, :], in_=parts[part]["v_ps"][:])
+
+        def park_v(part):
+            if not 0 <= part < N_PARTS:
+                return
+            b, g = divmod(part, J)
+            v_near = seqs[b]["v_near"]
             rows = out[b].rearrange("(m r) h -> m r h", r=R)[:, R - LW : R, :]
             nc.sync.dma_start(out=rows[g * P : (g + 1) * P], in_=v_near[:, g, R : R + LW, :])
 
@@ -315,13 +329,20 @@ def tile_singlehead_pa_t_kernel(tc, q, k_proj, x, Wv, out):
             step, turn = divmod(tile, J)
             return step, step // R, R - 1 - step % R, TILE_ORDER[turn]
 
+        def keep_clock(place, missing):
+            for extra in range(missing // P):
+                nc.tensor.matmul_mx(
+                    out=place[:, 0:P], lhsT=wv_codes[:].bitcast(FP8X4), lhsT_scale=wv_scales[:],
+                    rhs=wv_codes[:].bitcast(FP8X4), rhs_scale=wv_scales[:], start=True, stop=True,
+                )
+
         def logits(tile):
             if not 0 <= tile < N_TILES:
                 return
             step, b, r, j = where(tile)
             qk_t = seqs[b]["qk_t"]
             keys = (j + 1) * P
-            s_ps = psum_s.tile([P, M], F32)
+            s_ps = logit_places[j]
             nc.tensor.matmul(
                 out=s_ps[:, 0:keys], lhsT=qk_t[:, 0, r, KPAD + j * P : KPAD + keys],
                 rhs=qk_t[:, 1, KEY_ROWS.index(r), KPAD : KPAD + keys], start=True, stop=False,
@@ -335,7 +356,6 @@ def tile_singlehead_pa_t_kernel(tc, q, k_proj, x, Wv, out):
                 out=s_ps[:, j * P : keys], lhsT=mask_tiles[:, mask_row, :], rhs=ident_f32[:],
                 is_transpose=True, start=False, stop=True,
             )
-            logit_tiles[tile] = s_ps
 
         def negated_top(tile):
             if not 0 <= tile < N_TILES:
@@ -349,7 +369,7 @@ def tile_singlehead_pa_t_kernel(tc, q, k_proj, x, Wv, out):
                 )
             minus_s = work.tile([P, M], BF16)
             nc.vector.tensor_scalar(
-                out=minus_s[:, 0 : (j + 1) * P], in0=logit_tiles[tile][:, 0 : (j + 1) * P], scalar1=-SCALE,
+                out=minus_s[:, 0 : (j + 1) * P], in0=logit_places[j][:, 0 : (j + 1) * P], scalar1=-SCALE,
                 scalar2=seqs[b]["near_min"][:, r, j : j + 1], op0=ALU.mult, op1=ALU.min,
                 accum_out=steps[step]["neg_top"][:, j : j + 1],
             )
@@ -364,7 +384,7 @@ def tile_singlehead_pa_t_kernel(tc, q, k_proj, x, Wv, out):
             if pairs > 0:
                 nc.scalar.activation(
                     out=e_rows[:, 0:pairs].rearrange("p (u w e) -> p u w e", e=2, w=P),
-                    in_=logit_tiles[tile][:, 0:pairs].rearrange("p (u e w) -> p u w e", e=2, w=P),
+                    in_=logit_places[j][:, 0:pairs].rearrange("p (u e w) -> p u w e", e=2, w=P),
                     func=ACT.Exp, bias=neg_top, scale=SCALE,
                     accum_out=steps[step]["e_sums"][:, j, LW : LW + 1],
                 )
@@ -372,7 +392,7 @@ def tile_singlehead_pa_t_kernel(tc, q, k_proj, x, Wv, out):
                 column = LW + (1 if pairs > 0 else 0)
                 nc.scalar.activation(
                     out=e_rows[:, pairs:].rearrange("p (w e) -> p w e", e=2)[:, :, 0],
-                    in_=logit_tiles[tile][:, pairs : pairs + P],
+                    in_=logit_places[j][:, pairs : pairs + P],
                     func=ACT.Exp, bias=neg_top, scale=SCALE,
                     accum_out=steps[step]["e_sums"][:, j, column : column + 1],
                 )
@@ -493,55 +513,68 @@ def tile_singlehead_pa_t_kernel(tc, q, k_proj, x, Wv, out):
                         in1=share[:, j, :], op0=ALU.mult, op1=ALU.add,
                     )
 
-        def result(step):
+        def result(step, tiles):
             if not 0 <= step < N_STEPS:
                 return
             b, r = step // R, R - 1 - step % R
             o_sb, share = seqs[b]["o_sb"], steps[step]["share"]
-            for j in range(J):
+            for j in tiles:
                 nc.vector.scalar_tensor_tensor(
                     out=o_sb[:, j, r, :], in0=steps[step]["o_ps"][:, j, :],
                     scalar=steps[step]["inv_den"][:, j : j + 1], in1=share[:, j, :],
                     op0=ALU.mult, op1=ALU.add,
                 )
-            if r == 0:
-                nc.sync.dma_start(out=out[b].rearrange("(j p r) h -> p j r h", j=J, r=R), in_=o_sb[:])
 
-        load(0)
-        for step in range(-R, N_STEPS + 2):
+        def store(step):
+            if not 0 <= step < N_STEPS or step % R != R - 1:
+                return
+            b = step // R
+            nc.sync.dma_start(out=out[b].rearrange("(j p r) h -> p j r h", j=J, r=R), in_=seqs[b]["o_sb"][:])
+
+        load_qk(0)
+        load_x(0)
+        load_qk(1)
+        for step in range(-R - 1, N_STEPS + 2):
             part = step + R
             for j in range(J):
                 tile = step * J + j
-                if j == 0:
-                    local_minimum(part - 1)
-                logits(tile + 3)
+                owner = (part, step - 1, part, part + 1)[j]
+                others = R * P if 0 <= owner < (N_STEPS if j == 1 else N_PARTS) else 0
+                ahead = TILE_ORDER[j]
+                own = (ahead + 1) * P if 0 <= tile + 4 < N_TILES else 0
+                keep_clock(logit_places[ahead], (FILL if tile >= 0 else FILL_ALONE) - own - others)
+                logits(tile + 4)
                 negated_top(tile + 3)
                 exponentials(tile + 1)
                 keys_to_partitions(tile)
                 if j == 0:
-                    load(part + 1)
-                    heads_to_partitions(part)
-                    x_to_partitions(part, 0)
+                    load_x(part + 1)
+                    load_qk(part + 2)
+                    park_v(part - 1)
+                    x_to_partitions(part, 1)
+                    local_dots(part, 0)
                     quantise_e_and_v(step - 1)
                     inverse_denominator(step - 1)
                 if j == 1:
-                    fetch_v_before(part - 2)
-                    project(part - 1)
-                    keep_v(part - 1)
-                    group_queries(part)
-                    local_weights(step - 1)
-                if j == 2:
+                    store(step - 2)
+                    heads_to_partitions(part + 1)
                     atrous_sum(step - 1)
-                    x_to_partitions(part, 1)
-                    local_dots(part, 0)
-                    local_dots(part, 1)
+                    own_columns(part)
+                    local_weights(step - 1)
+                    quantise_x(part)
                     local_share(step - 1, 2)
+                if j == 2:
+                    fetch_v_before(part - 1)
+                    project(part)
+                    keep_v(part)
+                    group_queries(part + 1)
+                    local_logits(part)
                     local_exponentials(step)
                     local_share(step - 1, 1)
                 if j == 3:
-                    own_columns(part)
+                    x_to_partitions(part + 1, 0)
+                    local_dots(part + 1, 1)
                     group_v(step)
-                    quantise_x(part)
-                    local_logits(part)
+                    local_minimum(part)
                     denominator(step)
-                    result(step - 1)
+                    result(step - 1, range(J))

@@ -40,8 +40,6 @@ N_NEAR_MASKS = 2
 KEY0_COLS = 2
 TILE_ORDER = (0, 2, 1, 3)
 
-FILL, FILL_ALONE = 1024, 768
-
 N_PARTS = B * J
 N_STEPS = B * R
 N_TILES = N_STEPS * J
@@ -329,13 +327,6 @@ def tile_singlehead_pa_t_kernel(tc, q, k_proj, x, Wv, out):
             step, turn = divmod(tile, J)
             return step, step // R, R - 1 - step % R, TILE_ORDER[turn]
 
-        def keep_clock(place, missing):
-            for extra in range(missing // P):
-                nc.tensor.matmul_mx(
-                    out=place[:, 0:P], lhsT=wv_codes[:].bitcast(FP8X4), lhsT_scale=wv_scales[:],
-                    rhs=wv_codes[:].bitcast(FP8X4), rhs_scale=wv_scales[:], start=True, stop=True,
-                )
-
         def logits(tile):
             if not 0 <= tile < N_TILES:
                 return
@@ -538,11 +529,6 @@ def tile_singlehead_pa_t_kernel(tc, q, k_proj, x, Wv, out):
             part = step + R
             for j in range(J):
                 tile = step * J + j
-                owner = (part, step - 1, part, part + 1)[j]
-                others = R * P if 0 <= owner < (N_STEPS if j == 1 else N_PARTS) else 0
-                ahead = TILE_ORDER[j]
-                own = (ahead + 1) * P if 0 <= tile + 4 < N_TILES else 0
-                keep_clock(logit_places[ahead], (FILL if tile >= 0 else FILL_ALONE) - own - others)
                 logits(tile + 4)
                 negated_top(tile + 3)
                 exponentials(tile + 1)

@@ -52,7 +52,7 @@ def tile_singlehead_pa_t_kernel(tc, q, k_proj, x, Wv, out):
     with ExitStack() as ctx:
         ctx.enter_context(tc.manual_schedule())
         const = ctx.enter_context(tc.tile_pool(name="const", bufs=1))
-        loads = ctx.enter_context(tc.tile_pool(name="loads", bufs=3))
+        loads = ctx.enter_context(tc.tile_pool(name="loads", bufs=4))
         whole = ctx.enter_context(tc.tile_pool(name="whole", bufs=2))
         work = ctx.enter_context(tc.tile_pool(name="work", bufs=2))
         small = ctx.enter_context(tc.tile_pool(name="small", bufs=4))
@@ -128,13 +128,7 @@ def tile_singlehead_pa_t_kernel(tc, q, k_proj, x, Wv, out):
         ]
         for e_rows in e_rows_pair:
             for j in range(0, J, 2):
-                nc.vector.memset(e_rows[j][:, j * P :], 0.0)
-        e_sums_pair = [
-            const.tile([P, J, LW + 2], F32, name="e_sums_0"),
-            const.tile([P, J, LW + 2], F32, name="e_sums_1"),
-        ]
-        for e_sums in e_sums_pair:
-            nc.vector.memset(e_sums[:], 0.0)
+                nc.vector.memset(e_rows[j][:, (j + 1) * P :], 0.0)
         e_words_t = [psum_e.tile([P, 2, 2, P], F32, name="e_words_t_%d" % half) for half in range(2)]
         zeros_f32 = const.tile([P, P], F32)
         nc.vector.memset(zeros_f32[:], 0.0)
@@ -162,31 +156,37 @@ def tile_singlehead_pa_t_kernel(tc, q, k_proj, x, Wv, out):
             if not 0 <= part < N_PARTS:
                 return
             b, g = divmod(part, J)
-            tokens = slice(g * R * P, (g + 1) * R * P)
+            u, e = divmod(g, 2)
             x_in = loads.tile([P, R * D], BF16)
-            nc.sync.dma_start(out=x_in[:], in_=x[b, tokens, :].rearrange("(p r) d -> p (r d)", r=R))
+            nc.sync.dma_start(
+                out=x_in[:], in_=x[b].rearrange("(u p e r) d -> u p e (r d)", u=2, e=2, r=R)[u, :, e, :]
+            )
             parts[part]["x_in"] = x_in
 
-        def heads_to_partitions(part):
+        def heads_to_partitions(part, early=False):
             if not 0 <= part < N_PARTS:
                 return
             b, g = divmod(part, J)
             if g == 0:
                 seqs[b] = dict(
                     qk_t=qk_t_pair[b % 2],
-                    v_near=whole.tile([P, J, LW + R, H], F32, bufs=3, name="v_near"),
+                    v_keys=whole.tile([P, J, R, H], F32, name="v_keys"),
+                    v_near=whole.tile([P, J, LW + R, H], F32, name="v_near"),
                     near=whole.tile([P, LW, R, J], F32, name="near"),
                     near_min=whole.tile([P, R, J], F32, name="near_min"),
                     o_sb=whole.tile([P, J, R, H], F32, name="o_sb"),
                 )
             qk_in = parts[part]["qk_in"]
-            heads_t = psum_p.tile([P, 2, R, P], BF16, tag="prep")
+            if early:
+                heads_t = banks[part % 2 * 2][:].bitcast(BF16).rearrange("h (side r p) -> h side r p", side=2, r=R)
+            else:
+                heads_t = psum_p.tile([P, 2, R, P], BF16, tag="prep", name="heads_t")[:]
             for r in range(R):
                 nc.tensor.transpose(heads_t[:, 0, r, :], qk_in[:, 0, r, :], ident_bf[:])
             for row in range(R):
                 nc.tensor.transpose(heads_t[:, 1, row, :], qk_in[:, 1, KEY_ROWS[row], :], ident_bf[:])
             first = KPAD + g * P
-            nc.scalar.copy(out=seqs[b]["qk_t"][:, :, :, first : first + P], in_=heads_t[:])
+            nc.scalar.copy(out=seqs[b]["qk_t"][:, :, :, first : first + P], in_=heads_t)
 
         def group_queries(part):
             if not 0 <= part < N_PARTS:
@@ -253,7 +253,7 @@ def tile_singlehead_pa_t_kernel(tc, q, k_proj, x, Wv, out):
                 out=seqs[b]["near_min"][:, :, g], in0=near[:, 0, :, g], in1=near[:, 1, :, g], op=ALU.min
             )
 
-        def x_to_partitions(part, pair):
+        def x_to_partitions(part, pair, early=False):
             if not 0 <= part < N_PARTS:
                 return
             if pair == 0:
@@ -263,10 +263,11 @@ def tile_singlehead_pa_t_kernel(tc, q, k_proj, x, Wv, out):
             x_t = psum_p.tile([P, 2, 2, P], F32, tag="prep")
             for c in range(2):
                 transpose_words(x_t[:, c], x_words[:, 2 * pair + c])
-            nc.scalar.copy(
-                out=x_grouped_words[:, 2 * pair : 2 * pair + 2, :, :],
-                in_=x_t[:].rearrange("w c u p -> w c p u"),
-            )
+            out, in_ = x_grouped_words[:, 2 * pair : 2 * pair + 2, :, :], x_t[:].rearrange("w c u p -> w c p u")
+            if early and pair == 1:
+                nc.vector.tensor_copy(out=out, in_=in_)
+            else:
+                nc.scalar.copy(out=out, in_=in_)
 
         def quantise_x(part):
             if not 0 <= part < N_PARTS:
@@ -300,28 +301,29 @@ def tile_singlehead_pa_t_kernel(tc, q, k_proj, x, Wv, out):
             if not 0 <= part < N_PARTS:
                 return
             b, g = divmod(part, J)
-            v_near = seqs[b]["v_near"]
-            nc.scalar.copy(out=v_near[:, g, LW : LW + R, :], in_=parts[part]["v_ps"][:])
+            nc.scalar.copy(out=seqs[b]["v_keys"][:, g], in_=parts[part]["v_ps"][:])
 
         def park_v(part):
             if not 0 <= part < N_PARTS:
                 return
             b, g = divmod(part, J)
-            v_near = seqs[b]["v_near"]
-            rows = out[b].rearrange("(m r) h -> m r h", r=R)[:, R - LW : R, :]
-            nc.sync.dma_start(out=rows[g * P : (g + 1) * P], in_=v_near[:, g, R : R + LW, :])
+            u, e = divmod(g, 2)
+            nc.sync.dma_start(
+                out=out[b].rearrange("(u p e r) h -> u p e r h", u=2, e=2, r=R)[u, :, e], in_=seqs[b]["v_keys"][:, g]
+            )
 
-        def fetch_v_before(part):
-            if not 0 <= part < N_PARTS:
+        def fetch_v(b, j):
+            if not 0 <= b < B:
                 return
-            b, g = divmod(part, J)
             v_near = seqs[b]["v_near"]
-            rows = out[b].rearrange("(m r) h -> m r h", r=R)[:, R - LW : R, :]
-            if g == 0:
+            rows = out[b].rearrange("(p r) h -> p r h", r=R)[j * P : (j + 1) * P]
+            before = out[b].rearrange("(p r) h -> p r h", r=R)[:, R - LW : R, :]
+            nc.sync.dma_start(out=v_near[:, j, LW:, :], in_=rows)
+            if j == 0:
                 nc.vector.memset(v_near[0:1, 0, 0:LW, :], 0.0)
-                nc.sync.dma_start(out=v_near[1:P, 0, 0:LW, :], in_=rows[0 : P - 1])
+                nc.sync.dma_start(out=v_near[1:P, 0, 0:LW, :], in_=before[0 : P - 1])
             else:
-                nc.sync.dma_start(out=v_near[:, g, 0:LW, :], in_=rows[g * P - 1 : (g + 1) * P - 1])
+                nc.sync.dma_start(out=v_near[:, j, 0:LW, :], in_=before[j * P - 1 : (j + 1) * P - 1])
 
         def where(tile):
             step, turn = divmod(tile, J)
@@ -355,7 +357,7 @@ def tile_singlehead_pa_t_kernel(tc, q, k_proj, x, Wv, out):
             if tile % J == 0:
                 steps[step] = dict(
                     neg_top=small.tile([P, J], F32, name="neg_top"),
-                    e_sums=e_sums_pair[step % 2],
+                    e_sums=small.tile([P, J, LW + 1], F32, name="e_sums"),
                     e_grouped=work.tile([P, J, P, PACK], BF16, align_bytes=64, name="e_grouped"),
                 )
             minus_s = work.tile([P, M], BF16)
@@ -369,24 +371,12 @@ def tile_singlehead_pa_t_kernel(tc, q, k_proj, x, Wv, out):
             if not 0 <= tile < N_TILES:
                 return
             step, b, r, j = where(tile)
-            e_rows = e_rows_pair[step % 2][j]
-            pairs = (j + 1) // 2 * 2 * P
-            neg_top = steps[step]["neg_top"][:, j : j + 1]
-            if pairs > 0:
-                nc.scalar.activation(
-                    out=e_rows[:, 0:pairs].rearrange("p (u w e) -> p u w e", e=2, w=P),
-                    in_=logit_places[j][:, 0:pairs].rearrange("p (u e w) -> p u w e", e=2, w=P),
-                    func=ACT.Exp, bias=neg_top, scale=SCALE,
-                    accum_out=steps[step]["e_sums"][:, j, LW : LW + 1],
-                )
-            if j % 2 == 0:
-                column = LW + (1 if pairs > 0 else 0)
-                nc.scalar.activation(
-                    out=e_rows[:, pairs:].rearrange("p (w e) -> p w e", e=2)[:, :, 0],
-                    in_=logit_places[j][:, pairs : pairs + P],
-                    func=ACT.Exp, bias=neg_top, scale=SCALE,
-                    accum_out=steps[step]["e_sums"][:, j, column : column + 1],
-                )
+            keys = (j + 1) * P
+            nc.scalar.activation(
+                out=e_rows_pair[step % 2][j][:, 0:keys], in_=logit_places[j][:, 0:keys], func=ACT.Exp,
+                bias=steps[step]["neg_top"][:, j : j + 1], scale=SCALE,
+                accum_out=steps[step]["e_sums"][:, j, LW : LW + 1],
+            )
 
         def keys_to_partitions(tile):
             if not 0 <= tile < N_TILES:
@@ -419,7 +409,7 @@ def tile_singlehead_pa_t_kernel(tc, q, k_proj, x, Wv, out):
             b, r = step // R, R - 1 - step % R
             v_grouped = work.tile([P, H, PACK], BF16, align_bytes=64)
             nc.scalar.copy(
-                out=v_grouped[:], in_=seqs[b]["v_near"][:, :, LW + r, :].rearrange("p t h -> p h t")
+                out=v_grouped[:], in_=seqs[b]["v_keys"][:, :, r, :].rearrange("p t h -> p h t")
             )
             steps[step]["v_grouped"] = v_grouped
 
@@ -522,10 +512,29 @@ def tile_singlehead_pa_t_kernel(tc, q, k_proj, x, Wv, out):
             b = step // R
             nc.sync.dma_start(out=out[b].rearrange("(j p r) h -> p j r h", j=J, r=R), in_=seqs[b]["o_sb"][:])
 
-        load_qk(0)
-        load_x(0)
-        load_qk(1)
-        for step in range(-R - 1, N_STEPS + 2):
+        for part in range(R):
+            load_qk(part)
+            load_x(part)
+        heads_to_partitions(0, early=True)
+        for part in range(R):
+            group_queries(part)
+            x_to_partitions(part, 0, early=True)
+            if part < R - 1:
+                x_to_partitions(part, 1, early=True)
+                heads_to_partitions(part + 1, early=True)
+            local_dots(part, 1)
+            if part < R - 1:
+                local_dots(part, 0)
+                quantise_x(part)
+                own_columns(part)
+                project(part)
+                local_logits(part)
+                keep_v(part)
+                if part < R - 2:
+                    park_v(part)
+                local_minimum(part)
+        load_qk(R)
+        for step in range(-1, N_STEPS + 2):
             part = step + R
             for j in range(J):
                 tile = step * J + j
@@ -550,7 +559,9 @@ def tile_singlehead_pa_t_kernel(tc, q, k_proj, x, Wv, out):
                     quantise_x(part)
                     local_share(step - 1, 2)
                 if j == 2:
-                    fetch_v_before(part - 1)
+                    if step % R == 0:
+                        for tile_j in range(J):
+                            fetch_v(step // R, tile_j)
                     project(part)
                     keep_v(part)
                     group_queries(part + 1)

@@ -38,7 +38,7 @@ OWN_COLUMN = 0
 FIRST_TOKENS = 1
 N_NEAR_MASKS = 2
 KEY0_COLS = 2
-TILE_ORDER = (0, 2, 1, 3)
+TILE_ORDER = (1, 0, 2, 3)
 
 N_PARTS = B * J
 N_STEPS = B * R
@@ -129,15 +129,13 @@ def tile_singlehead_pa_t_kernel(tc, q, k_proj, x, Wv, out):
         for e_rows in e_rows_pair:
             for j in range(0, J, 2):
                 nc.vector.memset(e_rows[j][:, (j + 1) * P :], 0.0)
-        e_words_t = [psum_e.tile([P, 2, 2, P], F32, name="e_words_t_%d" % half) for half in range(2)]
+        e_words_t = psum_e.tile([P, 2, 2, P], F32)
         zeros_f32 = const.tile([P, P], F32)
         nc.vector.memset(zeros_f32[:], 0.0)
-        for odd in range(2):
-            nc.tensor.transpose(e_words_t[0][:, odd, 1, :], zeros_f32[:], ident_f32[:])
 
-        banks = [psum_s.tile([P, M], F32, name="logits_%d" % n) for n in range(3)]
+        banks = [psum_s.tile([P, M], F32, name="logits_%d" % n) for n in range(4)]
         logit_places = [banks[0][:, 0:P], banks[1][:, 0 : 2 * P], banks[0][:, P:M], banks[2][:]]
-        near_ps = banks[1][:, 2 * P : M].rearrange("p (r d c) -> p r d c", r=R, d=LW)
+        near_ps = banks[3][:, 0 : 2 * P].rearrange("p (r d c) -> p r d c", r=R, d=LW)
         seqs = {}
         parts = {}
         steps = {}
@@ -383,7 +381,7 @@ def tile_singlehead_pa_t_kernel(tc, q, k_proj, x, Wv, out):
                 return
             step, b, r, j = where(tile)
             words = e_rows_pair[step % 2][j][:].bitcast(F32)
-            words_t = e_words_t[j // 2][:, j % 2]
+            words_t = e_words_t[:, j // 2]
             for u in range(j // 2 + 1):
                 nc.tensor.transpose(words_t[:, u, :], words[:, u * P : (u + 1) * P], ident_f32[:])
             nc.scalar.copy(
@@ -534,6 +532,7 @@ def tile_singlehead_pa_t_kernel(tc, q, k_proj, x, Wv, out):
                     park_v(part)
                 local_minimum(part)
         load_qk(R)
+        nc.tensor.transpose(e_words_t[:, 0, 1, :], zeros_f32[:], ident_f32[:])
         for step in range(-1, N_STEPS + 2):
             part = step + R
             for j in range(J):

@@ -110,17 +110,18 @@ def tile_singlehead_pa_t_kernel(tc, q, k_proj, x, Wv, out):
                 nc.tensor.transpose(words_out[:, u, :], words_in[:, u, :], ident_f32[:])
 
         wv_sb = const.tile([P, D], BF16)
-        nc.sync.dma_start(out=wv_sb[:], in_=Wv)
-        wv_t = psum_p.tile([P, 2, P], F32, tag="prep")
-        transpose_words(wv_t, wv_sb[:].bitcast(F32).rearrange("h (u w) -> h u w", u=2))
-        wv_grouped = const.tile([P, H * PACK], BF16, align_bytes=64)
-        nc.vector.tensor_copy(
-            out=wv_grouped[:].bitcast(F32).rearrange("w (h u) -> w h u", u=2),
-            in_=wv_t[:].rearrange("w u h -> w h u"),
-        )
         wv_codes = const.tile([P, H], U32, align_bytes=64)
         wv_scales = const.tile([P, H], U8, align_bytes=64)
-        nc.vector.quantize_mx(out=wv_codes[:].bitcast(FP8X4), scales=wv_scales[:], in_=wv_grouped[:])
+
+        def quantise_wv():
+            wv_t = psum_p.tile([P, 2, P], F32, tag="prep")
+            transpose_words(wv_t, wv_sb[:].bitcast(F32).rearrange("h (u w) -> h u w", u=2))
+            wv_grouped = const.tile([P, H * PACK], BF16, align_bytes=64)
+            nc.vector.tensor_copy(
+                out=wv_grouped[:].bitcast(F32).rearrange("w (h u) -> w h u", u=2),
+                in_=wv_t[:].rearrange("w u h -> w h u"),
+            )
+            nc.vector.quantize_mx(out=wv_codes[:].bitcast(FP8X4), scales=wv_scales[:], in_=wv_grouped[:])
 
         e_rows_pair = [
             [const.tile([P, (j // 2 + 1) * 2 * P], BF16, name="e_rows_%d_%d" % (side, j)) for j in range(J)]
@@ -279,10 +280,13 @@ def tile_singlehead_pa_t_kernel(tc, q, k_proj, x, Wv, out):
             )
             parts[part]["x_codes"], parts[part]["x_scales"] = x_codes, x_scales
 
-        def project(part):
+        def project(part, early=False):
             if not 0 <= part < N_PARTS:
                 return
-            v_ps = psum_p.tile([P, R, H], F32, tag="prep")
+            if early:
+                v_ps = psum_o.tile([P, R, H], F32, name="o_ps")
+            else:
+                v_ps = psum_p.tile([P, R, H], F32, tag="prep", name="v_ps")
             for r in range(R):
                 nc.tensor.matmul_mx(
                     out=v_ps[:, r, :],
@@ -459,7 +463,7 @@ def tile_singlehead_pa_t_kernel(tc, q, k_proj, x, Wv, out):
             if not 0 <= step < N_STEPS:
                 return
             e_codes, e_scales, v_codes, v_scales = steps[step]["codes"]
-            o_ps = psum_o.tile([P, J, H], F32)
+            o_ps = psum_o.tile([P, J, H], F32, name="o_ps")
             for j in range(J):
                 nc.tensor.matmul_mx(
                     out=o_ps[:, j, :],
@@ -505,27 +509,42 @@ def tile_singlehead_pa_t_kernel(tc, q, k_proj, x, Wv, out):
                 )
 
         def store(step):
-            if not 0 <= step < N_STEPS or step % R != R - 1:
+            if not 0 <= step < N_STEPS:
                 return
-            b = step // R
-            nc.sync.dma_start(out=out[b].rearrange("(j p r) h -> p j r h", j=J, r=R), in_=seqs[b]["o_sb"][:])
+            b, r = step // R, R - 1 - step % R
+            if b == B - 1:
+                classes = slice(r, r + 1)
+            elif r == 0:
+                classes = slice(0, R)
+            else:
+                return
+            nc.sync.dma_start(
+                out=out[b].rearrange("(j p r) h -> p j r h", j=J, r=R)[:, :, classes, :],
+                in_=seqs[b]["o_sb"][:, :, classes, :],
+            )
 
-        for part in range(R):
+        load_qk(0)
+        load_x(0)
+        nc.sync.dma_start(out=wv_sb[:], in_=Wv)
+        for part in range(1, R):
             load_qk(part)
             load_x(part)
         heads_to_partitions(0, early=True)
+        group_queries(0)
         for part in range(R):
-            group_queries(part)
             x_to_partitions(part, 0, early=True)
             if part < R - 1:
                 x_to_partitions(part, 1, early=True)
+                if part == 0:
+                    quantise_wv()
                 heads_to_partitions(part + 1, early=True)
             local_dots(part, 1)
             if part < R - 1:
                 local_dots(part, 0)
                 quantise_x(part)
+                group_queries(part + 1)
                 own_columns(part)
-                project(part)
+                project(part, early=True)
                 local_logits(part)
                 keep_v(part)
                 if part < R - 2:

from contextlib import ExitStack
import math

import concourse.mybir as mybir
from concourse.masks import make_identity

F32 = mybir.dt.float32
BF16 = mybir.dt.bfloat16
U32 = mybir.dt.uint32
U8 = mybir.dt.uint8
FP8X4 = mybir.dt.float8_e4m3fn_x4
ALU = mybir.AluOpType
ACT = mybir.ActivationFunctionType
AX = mybir.AxisListType

B, S, D, H = 8, 2048, 512, 128
P = 128
PACK = 4
R = 4
LW = 2
M = S // R
J = M // P
SCALE = 1.0 / math.sqrt(D)
NEG = -1.0e30
KPAD = 16
KROW = KPAD + M

GROUP = 32
GROUPS = P // GROUP
ZSTEP = P + GROUP
ZROW = GROUPS * ZSTEP
KEY_ROWS = (2, 3, 0, 1)

CAUSAL = 0
CAUSAL_NO_KEY0 = 1
N_MASKS = 2
OWN_COLUMN = 0
FIRST_TOKENS = 1
N_NEAR_MASKS = 2
KEY0_COLS = 2
TILE_ORDER = (1, 0, 2, 3)

N_PARTS = B * J
N_STEPS = B * R
N_TILES = N_STEPS * J

FLOPS = 2 * B * S * D * H + 2 * (2 * B * R * M * M * H)


def tile_singlehead_pa_t_kernel(tc, q, k_proj, x, Wv, out):
    nc = tc.nc
    with ExitStack() as ctx:
        ctx.enter_context(tc.manual_schedule())
        const = ctx.enter_context(tc.tile_pool(name="const", bufs=1))
        loads = ctx.enter_context(tc.tile_pool(name="loads", bufs=4))
        whole = ctx.enter_context(tc.tile_pool(name="whole", bufs=2))
        work = ctx.enter_context(tc.tile_pool(name="work", bufs=2))
        small = ctx.enter_context(tc.tile_pool(name="small", bufs=4))
        psum_s = ctx.enter_context(tc.psum_pool(name="psum_s", bufs=1))
        psum_e = ctx.enter_context(tc.psum_pool(name="psum_e", bufs=1))
        psum_o = ctx.enter_context(tc.psum_pool(name="psum_o", bufs=1))
        psum_p = ctx.enter_context(tc.psum_pool(name="psum_p", bufs=2))

        ident_f32 = const.tile([P, P], F32)
        make_identity(nc, ident_f32[:])
        ident_bf = const.tile([P, P], BF16)
        make_identity(nc, ident_bf[:])

        causal_f32 = const.tile([P, P], F32)
        nc.gpsimd.memset(causal_f32[:], 0.0)
        nc.gpsimd.affine_select(
            out=causal_f32[:], in_=causal_f32[:], compare_op=ALU.is_ge, fill=NEG,
            base=0, pattern=[[1, P]], channel_multiplier=-1,
        )
        mask_tiles = const.tile([P, N_MASKS, P], F32)
        nc.vector.tensor_copy(out=mask_tiles[:, CAUSAL, :], in_=causal_f32[:])
        nc.vector.tensor_copy(out=mask_tiles[:, CAUSAL_NO_KEY0, :], in_=causal_f32[:])
        nc.vector.memset(mask_tiles[0:1, CAUSAL_NO_KEY0, 1:P], NEG)
        no_key0 = const.tile([P, KEY0_COLS], BF16)
        nc.vector.memset(no_key0[:], 0.0)
        nc.vector.memset(no_key0[:, 0:1], NEG)

        same_column = const.tile([P, GROUP], F32)
        nc.vector.tensor_reduce(
            out=same_column[:], in_=ident_f32[:].rearrange("p (a c) -> p c a", c=GROUP), axis=AX.X, op=ALU.add
        )
        near_masks = const.tile([P, N_NEAR_MASKS, GROUPS, GROUP], F32)
        for row in range(N_NEAR_MASKS):
            nc.vector.tensor_scalar(
                out=near_masks[:, row], in0=same_column[:].unsqueeze(1).to_broadcast([P, GROUPS, GROUP]),
                scalar1=-1.0, scalar2=-NEG, op0=ALU.add, op1=ALU.mult,
            )
        nc.vector.memset(near_masks[0 : 3 * GROUP, FIRST_TOKENS, 0, 0:1], NEG)

        qk_t_pair = [
            const.tile([P, 2, R, KROW], BF16, name="qk_t_0"),
            const.tile([P, 2, R, KROW], BF16, name="qk_t_1"),
        ]
        for qk_t in qk_t_pair:
            nc.vector.memset(qk_t[:, 1, :, 0:KPAD], 0.0)
        q_groups_pair = [
            const.tile([P, R, ZROW], BF16, name="q_groups_0"),
            const.tile([P, R, ZROW], BF16, name="q_groups_1"),
        ]
        for q_groups in q_groups_pair:
            nc.gpsimd.memset(q_groups[:].rearrange("h r c -> h (r c)").bitcast(F32), 0.0)

        def transpose_words(words_out, words_in):
            for u in range(2):
                nc.tensor.transpose(words_out[:, u, :], words_in[:, u, :], ident_f32[:])

        wv_sb = const.tile([P, D], BF16)
        wv_codes = const.tile([P, H], U32, align_bytes=64)
        wv_scales = const.tile([P, H], U8, align_bytes=64)

        def quantise_wv():
            wv_t = psum_p.tile([P, 2, P], F32, tag="prep")
            transpose_words(wv_t, wv_sb[:].bitcast(F32).rearrange("h (u w) -> h u w", u=2))
            wv_grouped = const.tile([P, H * PACK], BF16, align_bytes=64)
            nc.vector.tensor_copy(
                out=wv_grouped[:].bitcast(F32).rearrange("w (h u) -> w h u", u=2),
                in_=wv_t[:].rearrange("w u h -> w h u"),
            )
            nc.vector.quantize_mx(out=wv_codes[:].bitcast(FP8X4), scales=wv_scales[:], in_=wv_grouped[:])

        e_rows_pair = [
            [const.tile([P, (j // 2 + 1) * 2 * P], BF16, name="e_rows_%d_%d" % (side, j)) for j in range(J)]
            for side in range(2)
        ]
        for e_rows in e_rows_pair:
            for j in range(0, J, 2):
                nc.vector.memset(e_rows[j][:, (j + 1) * P :], 0.0)
        e_words_t = psum_e.tile([P, 2, 2, P], F32)
        zeros_f32 = const.tile([P, P], F32)
        nc.vector.memset(zeros_f32[:], 0.0)

        banks = [psum_s.tile([P, M], F32, name="logits_%d" % n) for n in range(4)]
        logit_places = [banks[0][:, 0:P], banks[1][:, 0 : 2 * P], banks[0][:, P:M], banks[2][:]]
        near_ps = banks[3][:, 0 : 2 * P].rearrange("p (r d c) -> p r d c", r=R, d=LW)
        seqs = {}
        parts = {}
        steps = {}

        def load_qk(part):
            if not 0 <= part < N_PARTS:
                return
            b, g = divmod(part, J)
            tokens = slice(g * R * P, (g + 1) * R * P)
            qk_in = loads.tile([P, 2, R, H], BF16)
            nc.sync.dma_start(out=qk_in[:, 0], in_=q[b, tokens, :].rearrange("(p r) h -> p r h", r=R))
            nc.sync.dma_start(out=qk_in[:, 1], in_=k_proj[b, tokens, :].rearrange("(p r) h -> p r h", r=R))
            parts[part] = dict(qk_in=qk_in)

        def load_x(part):
            if not 0 <= part < N_PARTS:
                return
            b, g = divmod(part, J)
            u, e = divmod(g, 2)
            x_in = loads.tile([P, R * D], BF16)
            nc.sync.dma_start(
                out=x_in[:], in_=x[b].rearrange("(u p e r) d -> u p e (r d)", u=2, e=2, r=R)[u, :, e, :]
            )
            parts[part]["x_in"] = x_in

        def heads_to_partitions(part, early=False):
            if not 0 <= part < N_PARTS:
                return
            b, g = divmod(part, J)
            if g == 0:
                seqs[b] = dict(
                    qk_t=qk_t_pair[b % 2],
                    v_keys=whole.tile([P, J, R, H], F32, name="v_keys"),
                    v_near=whole.tile([P, J, LW + R, H], F32, name="v_near"),
                    near=whole.tile([P, LW, R, J], F32, name="near"),
                    near_min=whole.tile([P, R, J], F32, name="near_min"),
                    o_sb=whole.tile([P, J, R, H], F32, name="o_sb"),
                )
            qk_in = parts[part]["qk_in"]
            if early:
                heads_t = banks[part % 2 * 2][:].bitcast(BF16).rearrange("h (side r p) -> h side r p", side=2, r=R)
            else:
                heads_t = psum_p.tile([P, 2, R, P], BF16, tag="prep", name="heads_t")[:]
            for r in range(R):
                nc.tensor.transpose(heads_t[:, 0, r, :], qk_in[:, 0, r, :], ident_bf[:])
            for row in range(R):
                nc.tensor.transpose(heads_t[:, 1, row, :], qk_in[:, 1, KEY_ROWS[row], :], ident_bf[:])
            first = KPAD + g * P
            nc.scalar.copy(out=seqs[b]["qk_t"][:, :, :, first : first + P], in_=heads_t)

        def group_queries(part):
            if not 0 <= part < N_PARTS:
                return
            b, g = divmod(part, J)
            first = KPAD + g * P
            nc.vector.tensor_copy(
                out=q_groups_pair[part % 2][:].rearrange("h r (gg s) -> h r gg s", s=ZSTEP)[:, :, :, 0:GROUP],
                in_=seqs[b]["qk_t"][:, 0, :, first : first + P].rearrange("h r (gg c) -> h r gg c", c=GROUP),
            )

        def local_keys(keys, r, column):
            if r == 0:
                return keys[:, 0:2, column - 1 : column - 1 + GROUP]
            if r == 1:
                step = KROW + 1
                first = KROW + column - 1
                flat = keys.rearrange("h row c -> h (row c)")[:, first : first + 2 * step]
                return flat.rearrange("h (d c) -> h d c", d=2)[:, :, 0:GROUP]
            if r == 2:
                return keys[:, 2:4, column : column + GROUP]
            return keys[:, 0:4:3, column : column + GROUP]

        def local_dots(part, pair):
            if not 0 <= part < N_PARTS:
                return
            b, g = divmod(part, J)
            row = FIRST_TOKENS if (g == 0 and pair == 0) else OWN_COLUMN
            nc.tensor.matmul(
                out=near_ps[:, 2 * pair : 2 * pair + 2].rearrange("p r d c -> p (r d c)"),
                lhsT=near_masks[:, row].rearrange("p gg c -> p (gg c)"), rhs=ident_f32[:],
                is_transpose=True, start=True, stop=False,
            )
            for r in (2 * pair, 2 * pair + 1):
                for gg in range(GROUPS):
                    nc.tensor.matmul(
                        out=near_ps[:, r], lhsT=q_groups_pair[part % 2][:, r, gg * P : (gg + 1) * P],
                        rhs=local_keys(seqs[b]["qk_t"][:, 1], r, KPAD + g * P + gg * GROUP),
                        start=False, stop=(r == 2 * pair + 1 and gg == GROUPS - 1),
                    )

        def own_columns(part):
            if not 0 <= part < N_PARTS:
                return
            near_raw = small.tile([P, R, LW], F32)
            nc.vector.tensor_reduce(out=near_raw[:], in_=near_ps, axis=AX.X, op=ALU.max)
            parts[part]["near_raw"] = near_raw

        def local_logits(part):
            if not 0 <= part < N_PARTS:
                return
            b, g = divmod(part, J)
            nc.vector.tensor_scalar_mul(
                out=seqs[b]["near"][:, :, :, g], in0=parts[part]["near_raw"][:].rearrange("p r d -> p d r"),
                scalar1=-SCALE,
            )

        def local_minimum(part):
            if not 0 <= part < N_PARTS:
                return
            b, g = divmod(part, J)
            near = seqs[b]["near"]
            nc.vector.tensor_tensor(
                out=seqs[b]["near_min"][:, :, g], in0=near[:, 0, :, g], in1=near[:, 1, :, g], op=ALU.min
            )

        def x_to_partitions(part, pair, early=False):
            if not 0 <= part < N_PARTS:
                return
            if pair == 0:
                parts[part]["x_grouped"] = work.tile([P, R * P * PACK], BF16, align_bytes=64, name="x_grouped")
            x_words = parts[part]["x_in"][:].bitcast(F32).rearrange("p (r u w) -> p r u w", r=R, u=2)
            x_grouped_words = parts[part]["x_grouped"][:].bitcast(F32).rearrange("w (r p u) -> w r p u", r=R, p=P)
            x_t = psum_p.tile([P, 2, 2, P], F32, tag="prep")
            for c in range(2):
                transpose_words(x_t[:, c], x_words[:, 2 * pair + c])
            out, in_ = x_grouped_words[:, 2 * pair : 2 * pair + 2, :, :], x_t[:].rearrange("w c u p -> w c p u")
            if early and pair == 1:
                nc.vector.tensor_copy(out=out, in_=in_)
            else:
                nc.scalar.copy(out=out, in_=in_)

        def quantise_x(part):
            if not 0 <= part < N_PARTS:
                return
            x_codes = work.tile([P, R, P], U32, align_bytes=64)
            x_scales = work.tile([P, R, P], U8, align_bytes=64)
            nc.vector.quantize_mx(
                out=x_codes[:].rearrange("w r p -> w (r p)").bitcast(FP8X4),
                scales=x_scales[:].rearrange("w r p -> w (r p)"),
                in_=parts[part]["x_grouped"][:],
            )
            parts[part]["x_codes"], parts[part]["x_scales"] = x_codes, x_scales

        def project(part, early=False):
            if not 0 <= part < N_PARTS:
                return
            if early:
                v_ps = psum_o.tile([P, R, H], F32, name="o_ps")
            else:
                v_ps = psum_p.tile([P, R, H], F32, tag="prep", name="v_ps")
            for r in range(R):
                nc.tensor.matmul_mx(
                    out=v_ps[:, r, :],
                    lhsT=parts[part]["x_codes"][:, r, :].bitcast(FP8X4),
                    lhsT_scale=parts[part]["x_scales"][:, r, :],
                    rhs=wv_codes[:].bitcast(FP8X4),
                    rhs_scale=wv_scales[:],
                    start=True,
                    stop=True,
                )
            parts[part]["v_ps"] = v_ps

        def keep_v(part):
            if not 0 <= part < N_PARTS:
                return
            b, g = divmod(part, J)
            nc.scalar.copy(out=seqs[b]["v_keys"][:, g], in_=parts[part]["v_ps"][:])

        def park_v(part):
            if not 0 <= part < N_PARTS:
                return
            b, g = divmod(part, J)
            u, e = divmod(g, 2)
            nc.sync.dma_start(
                out=out[b].rearrange("(u p e r) h -> u p e r h", u=2, e=2, r=R)[u, :, e], in_=seqs[b]["v_keys"][:, g]
            )

        def fetch_v(b, j):
            if not 0 <= b < B:
                return
            v_near = seqs[b]["v_near"]
            rows = out[b].rearrange("(p r) h -> p r h", r=R)[j * P : (j + 1) * P]
            before = out[b].rearrange("(p r) h -> p r h", r=R)[:, R - LW : R, :]
            nc.sync.dma_start(out=v_near[:, j, LW:, :], in_=rows)
            if j == 0:
                nc.vector.memset(v_near[0:1, 0, 0:LW, :], 0.0)
                nc.sync.dma_start(out=v_near[1:P, 0, 0:LW, :], in_=before[0 : P - 1])
            else:
                nc.sync.dma_start(out=v_near[:, j, 0:LW, :], in_=before[j * P - 1 : (j + 1) * P - 1])

        def where(tile):
            step, turn = divmod(tile, J)
            return step, step // R, R - 1 - step % R, TILE_ORDER[turn]

        def logits(tile):
            if not 0 <= tile < N_TILES:
                return
            step, b, r, j = where(tile)
            qk_t = seqs[b]["qk_t"]
            keys = (j + 1) * P
            s_ps = logit_places[j]
            nc.tensor.matmul(
                out=s_ps[:, 0:keys], lhsT=qk_t[:, 0, r, KPAD + j * P : KPAD + keys],
                rhs=qk_t[:, 1, KEY_ROWS.index(r), KPAD : KPAD + keys], start=True, stop=False,
            )
            if r == 0 and j > 0:
                nc.tensor.matmul(
                    out=s_ps[:, 0:KEY0_COLS], lhsT=ident_bf[:], rhs=no_key0[:], start=False, stop=False,
                )
            mask_row = CAUSAL_NO_KEY0 if (r == 0 and j == 0) else CAUSAL
            nc.tensor.matmul(
                out=s_ps[:, j * P : keys], lhsT=mask_tiles[:, mask_row, :], rhs=ident_f32[:],
                is_transpose=True, start=False, stop=True,
            )

        def negated_top(tile):
            if not 0 <= tile < N_TILES:
                return
            step, b, r, j = where(tile)
            if tile % J == 0:
                steps[step] = dict(
                    neg_top=small.tile([P, J], F32, name="neg_top"),
                    e_sums=small.tile([P, J, LW + 1], F32, name="e_sums"),
                    e_grouped=work.tile([P, J, P, PACK], BF16, align_bytes=64, name="e_grouped"),
                )
            minus_s = work.tile([P, M], BF16)
            nc.vector.tensor_scalar(
                out=minus_s[:, 0 : (j + 1) * P], in0=logit_places[j][:, 0 : (j + 1) * P], scalar1=-SCALE,
                scalar2=seqs[b]["near_min"][:, r, j : j + 1], op0=ALU.mult, op1=ALU.min,
                accum_out=steps[step]["neg_top"][:, j : j + 1],
            )

        def exponentials(tile):
            if not 0 <= tile < N_TILES:
                return
            step, b, r, j = where(tile)
            keys = (j + 1) * P
            nc.scalar.activation(
                out=e_rows_pair[step % 2][j][:, 0:keys], in_=logit_places[j][:, 0:keys], func=ACT.Exp,
                bias=steps[step]["neg_top"][:, j : j + 1], scale=SCALE,
                accum_out=steps[step]["e_sums"][:, j, LW : LW + 1],
            )

        def keys_to_partitions(tile):
            if not 0 <= tile < N_TILES:
                return
            step, b, r, j = where(tile)
            words = e_rows_pair[step % 2][j][:].bitcast(F32)
            words_t = e_words_t[:, j // 2]
            for u in range(j // 2 + 1):
                nc.tensor.transpose(words_t[:, u, :], words[:, u * P : (u + 1) * P], ident_f32[:])
            nc.scalar.copy(
                out=steps[step]["e_grouped"][:, j].rearrange("p m t -> p (m t)").bitcast(F32).rearrange(
                    "p (m u) -> p m u", u=2),
                in_=words_t.rearrange("p u m -> p m u"),
            )

        def local_exponentials(step):
            if not 0 <= step < N_STEPS:
                return
            b, r = step // R, R - 1 - step % R
            exponents = small.tile([P, J, LW], F32)
            nc.vector.tensor_tensor(
                out=exponents[:], in0=steps[step]["neg_top"][:].unsqueeze(2).to_broadcast([P, J, LW]),
                in1=seqs[b]["near"][:, :, r, :].rearrange("p d j -> p j d"), op=ALU.subtract,
            )
            nc.scalar.activation(out=steps[step]["e_sums"][:, :, 0:LW], in_=exponents[:], func=ACT.Exp)

        def group_v(step):
            if not 0 <= step < N_STEPS:
                return
            b, r = step // R, R - 1 - step % R
            v_grouped = work.tile([P, H, PACK], BF16, align_bytes=64)
            nc.scalar.copy(
                out=v_grouped[:], in_=seqs[b]["v_keys"][:, :, r, :].rearrange("p t h -> p h t")
            )
            steps[step]["v_grouped"] = v_grouped

        def denominator(step):
            if not 0 <= step < N_STEPS:
                return
            den = small.tile([P, J], F32)
            nc.vector.tensor_reduce(out=den[:], in_=steps[step]["e_sums"][:], axis=AX.X, op=ALU.add)
            steps[step]["den"] = den

        def inverse_denominator(step):
            if not 0 <= step < N_STEPS:
                return
            inv_den = small.tile([P, J], F32)
            nc.vector.reciprocal(out=inv_den[:], in_=steps[step]["den"][:])
            steps[step]["inv_den"] = inv_den

        def local_weights(step):
            if not 0 <= step < N_STEPS:
                return
            b, r = step // R, R - 1 - step % R
            e_sums, inv_den = steps[step]["e_sums"], steps[step]["inv_den"]
            w_near = small.tile([P, J, LW], F32)
            nc.vector.tensor_tensor(
                out=w_near[:], in0=e_sums[:, :, 0:LW],
                in1=inv_den[:].unsqueeze(2).to_broadcast([P, J, LW]), op=ALU.mult,
            )
            steps[step]["w_near"] = w_near

        def quantise_e_and_v(step):
            if not 0 <= step < N_STEPS:
                return
            e_codes = work.tile([P, J, P], U32, align_bytes=64)
            e_scales = work.tile([P, J, P], U8, align_bytes=64)
            nc.vector.quantize_mx(
                out=e_codes[:].rearrange("p j m -> p (j m)").bitcast(FP8X4),
                scales=e_scales[:].rearrange("p j m -> p (j m)"),
                in_=steps[step]["e_grouped"][:].rearrange("p j m t -> p (j m t)"),
            )
            v_codes = work.tile([P, H], U32, align_bytes=64)
            v_scales = work.tile([P, H], U8, align_bytes=64)
            nc.vector.quantize_mx(
                out=v_codes[:].bitcast(FP8X4), scales=v_scales[:],
                in_=steps[step]["v_grouped"][:].rearrange("p h t -> p (h t)"),
            )
            steps[step]["codes"] = (e_codes, e_scales, v_codes, v_scales)

        def atrous_sum(step):
            if not 0 <= step < N_STEPS:
                return
            e_codes, e_scales, v_codes, v_scales = steps[step]["codes"]
            o_ps = psum_o.tile([P, J, H], F32, name="o_ps")
            for j in range(J):
                nc.tensor.matmul_mx(
                    out=o_ps[:, j, :],
                    lhsT=e_codes[:, j, :].bitcast(FP8X4),
                    lhsT_scale=e_scales[:, j, :],
                    rhs=v_codes[:].bitcast(FP8X4),
                    rhs_scale=v_scales[:],
                    start=True,
                    stop=True,
                )
            steps[step]["o_ps"] = o_ps

        def local_share(step, d):
            if not 0 <= step < N_STEPS:
                return
            b, r = step // R, R - 1 - step % R
            v_near, w_near = seqs[b]["v_near"], steps[step]["w_near"]
            place = d - 1 if r == R - 1 else LW - d
            if d == LW:
                steps[step]["share"] = work.tile([P, J, H], F32, name="share")
            share = steps[step]["share"]
            for j in range(J):
                if d == LW:
                    nc.vector.tensor_scalar_mul(
                        out=share[:, j, :], in0=v_near[:, j, LW + r - d, :], scalar1=w_near[:, j, place : place + 1]
                    )
                else:
                    nc.vector.scalar_tensor_tensor(
                        out=share[:, j, :], in0=v_near[:, j, LW + r - d, :], scalar=w_near[:, j, place : place + 1],
                        in1=share[:, j, :], op0=ALU.mult, op1=ALU.add,
                    )

        def result(step, tiles):
            if not 0 <= step < N_STEPS:
                return
            b, r = step // R, R - 1 - step % R
            o_sb, share = seqs[b]["o_sb"], steps[step]["share"]
            for j in tiles:
                nc.vector.scalar_tensor_tensor(
                    out=o_sb[:, j, r, :], in0=steps[step]["o_ps"][:, j, :],
                    scalar=steps[step]["inv_den"][:, j : j + 1], in1=share[:, j, :],
                    op0=ALU.mult, op1=ALU.add,
                )

        def store(step):
            if not 0 <= step < N_STEPS:
                return
            b, r = step // R, R - 1 - step % R
            if b == B - 1:
                classes = slice(r, r + 1)
            elif r == 0:
                classes = slice(0, R)
            else:
                return
            nc.sync.dma_start(
                out=out[b].rearrange("(j p r) h -> p j r h", j=J, r=R)[:, :, classes, :],
                in_=seqs[b]["o_sb"][:, :, classes, :],
            )

        load_qk(0)
        load_x(0)
        nc.sync.dma_start(out=wv_sb[:], in_=Wv)
        for part in range(1, R):
            load_qk(part)
            load_x(part)
        heads_to_partitions(0, early=True)
        group_queries(0)
        for part in range(R):
            x_to_partitions(part, 0, early=True)
            if part < R - 1:
                x_to_partitions(part, 1, early=True)
                if part == 0:
                    quantise_wv()
                heads_to_partitions(part + 1, early=True)
            local_dots(part, 1)
            if part < R - 1:
                local_dots(part, 0)
                quantise_x(part)
                group_queries(part + 1)
                own_columns(part)
                project(part, early=True)
                local_logits(part)
                keep_v(part)
                if part < R - 2:
                    park_v(part)
                local_minimum(part)
        load_qk(R)
        nc.tensor.transpose(e_words_t[:, 0, 1, :], zeros_f32[:], ident_f32[:])
        for step in range(-1, N_STEPS + 2):
            part = step + R
            for j in range(J):
                tile = step * J + j
                logits(tile + 4)
                negated_top(tile + 3)
                exponentials(tile + 1)
                keys_to_partitions(tile)
                if j == 0:
                    load_x(part + 1)
                    load_qk(part + 2)
                    park_v(part - 1)
                    x_to_partitions(part, 1)
                    local_dots(part, 0)
                    quantise_e_and_v(step - 1)
                    inverse_denominator(step - 1)
                if j == 1:
                    store(step - 2)
                    heads_to_partitions(part + 1)
                    atrous_sum(step - 1)
                    own_columns(part)
                    local_weights(step - 1)
                    quantise_x(part)
                    local_share(step - 1, 2)
                if j == 2:
                    if step % R == 0:
                        for tile_j in range(J):
                            fetch_v(step // R, tile_j)
                    project(part)
                    keep_v(part)
                    group_queries(part + 1)
                    local_logits(part)
                    local_exponentials(step)
                    local_share(step - 1, 1)
                if j == 3:
                    x_to_partitions(part + 1, 0)
                    local_dots(part + 1, 1)
                    group_v(step)
                    local_minimum(part)
                    denominator(step)
                    result(step - 1, range(J))
